import numpy as np
import ml_dtypes


def mxq(x, axis, fmt="e4m3"):
    dtype, down = {"e4m3": (ml_dtypes.float8_e4m3fn, 7), "e5m2": (ml_dtypes.float8_e5m2, 14)}[fmt]
    v = np.moveaxis(np.asarray(x, np.float32).astype(ml_dtypes.bfloat16).astype(np.float64), axis, -1)
    blocks = v.reshape(v.shape[:-1] + (-1, 32))
    amax = np.abs(blocks).max(-1, keepdims=True)
    byte = np.maximum(np.where(amax > 0, np.frexp(amax)[1] - 1 + 127, 0) - down, 1)
    scale = np.exp2(byte - 127.0)
    codes = (blocks / scale).astype(np.float32).astype(dtype).astype(np.float64)
    return np.moveaxis((codes * scale).reshape(v.shape), -1, axis)


WIDE = False


def mx_kscale(k):
    if not WIDE:
        return np.ones(k)
    levels = np.array([10, -10, 5, -5, 0])
    if k % 512:
        return np.exp2(np.random.permutation(np.resize(levels, k // 32))).repeat(32)
    a = np.empty((k // 512, 16))
    for p in range(k // 512):
        a[p, :8] = np.random.permutation(np.resize(levels, 8))
        for g in range(8):
            far = levels[np.abs(levels - a[p, g]) >= 10]
            a[p, g + 8] = far[np.random.randint(len(far))]
    return np.exp2(a.ravel()).repeat(32)


BF16 = ml_dtypes.bfloat16


def bf(x):
    return np.asarray(x, np.float32).astype(BF16)


def f64(x):
    return np.asarray(x).astype(np.float64)


B, T, N, H, G, GH = 32, 4, 32, 512, 9, 3


def sigmoid(v):
    return 1.0 / (1.0 + np.exp(-v))


def setup_inputs():
    s = mx_kscale(H)
    return {"h_new": bf(np.random.standard_normal((B, T, N, H)) * 0.35 * s),
            "c_new": bf(np.random.standard_normal((B, T, N, H)) * 0.8),
            "g_s": bf(np.random.standard_normal((B, T, H)) * s),
            "c_g_s": bf(np.random.standard_normal((B, T, H)) * 0.5),
            "Wg_s": bf(np.random.standard_normal((GH, T, H, H)) * 2.0 / np.sqrt(H) / s[:, None]),
            "Zg_s": bf(np.random.standard_normal((GH, T, H, H)) * 1.0 / np.sqrt(H) / s[:, None]),
            "bg_s": bf(np.random.standard_normal((GH, T, 1, H)) * 0.3)}


def reference(h_new, c_new, g_s, c_g_s, Wg_s, Zg_s, bg_s):
    c_new, c_g_s = f64(c_new), f64(c_g_s)
    hq = mxq(f64(h_new).transpose(1, 0, 2, 3).reshape(T, B * N, H), 2, "e4m3")
    preg = (hq @ mxq(f64(Wg_s), 2, "e4m3")) + f64(bg_s)
    preg = preg.reshape(GH, T, B, N, H).transpose(0, 2, 1, 3, 4)
    zs_part = mxq(f64(g_s).transpose(1, 0, 2), 2, "e4m3") @ mxq(f64(Zg_s), 2, "e4m3")
    zs_part = zs_part.transpose(0, 2, 1, 3)[:, :, :, None]
    f_s, gg_s, o_s = sigmoid(preg + zs_part)
    c_g_s_new = np.mean(f_s * c_new, axis=2) + np.mean(gg_s, axis=2) * c_g_s
    g_s_new = np.mean(o_s, axis=2) * np.tanh(c_g_s_new)
    return g_s_new, c_g_s_new

@@ -1,0 +1,315 @@
+from contextlib import ExitStack
+
+import concourse.mybir as mybir
+from concourse.masks import make_identity
+
+F32 = mybir.dt.float32
+BF16 = mybir.dt.bfloat16
+U32 = mybir.dt.uint32
+U8 = mybir.dt.uint8
+FP8X4 = mybir.dt.float8_e4m3fn_x4
+ACT = mybir.ActivationFunctionType
+ALU = mybir.AluOpType
+
+P = 128
+PACK = 4
+SEQS = 32
+FRAMES = 4
+BONES = 32
+FEAT = 512
+GATES = 3
+F_GATE, GG_GATE, O_GATE = 0, 1, 2
+UNITS = FRAMES * GATES
+FEAT_TILES = FEAT // P
+BONE_ROWS = P // SEQS
+BONE_STEPS = BONES // BONE_ROWS
+WORDS = FEAT // 2
+COLS = BONES * SEQS
+BANK = 512
+HALVES = COLS // BANK
+BANK_BONES = BANK // SEQS
+AHEAD = 2
+SUM_LAG = 2
+
+FLOPS = 2 * GATES * FRAMES * FEAT * FEAT * (COLS + SEQS)
+
+
+def tile_st_hmr_pc_t_kernel(tc, h_new, c_new, g_s, c_g_s, Wg_s, Zg_s, bg_s, out_0, out_1):
+    nc = tc.nc
+    with ExitStack() as ctx:
+        const = ctx.enter_context(tc.tile_pool(name="const", bufs=1))
+        frames = ctx.enter_context(tc.tile_pool(name="frames", bufs=2))
+        raws = ctx.enter_context(tc.tile_pool(name="raws", bufs=AHEAD + 1))
+        stage = ctx.enter_context(tc.tile_pool(name="stage", bufs=2))
+        frame_ops = ctx.enter_context(tc.tile_pool(name="frame_ops", bufs=2))
+        weight_ops = ctx.enter_context(tc.tile_pool(name="weight_ops", bufs=AHEAD + 1))
+        gate_pool = ctx.enter_context(tc.tile_pool(name="gate_pool", bufs=SUM_LAG + 2))
+        mm = ctx.enter_context(tc.psum_pool(name="mm", bufs=4))
+        flip = ctx.enter_context(tc.psum_pool(name="flip", bufs=4))
+        ctx.enter_context(tc.manual_schedule())
+
+        ident_f32 = const.tile([P, P], F32)
+        make_identity(nc, ident_f32[:])
+        ident_bf = const.tile([P, P], BF16)
+        make_identity(nc, ident_bf[:])
+        sort_f32 = const.tile([P, P], F32)
+        nc.vector.tensor_copy(
+            out=sort_f32[:].rearrange("i (r b) -> i r b", r=BONE_ROWS),
+            in_=ident_f32[:].rearrange("i (b r) -> i r b", r=BONE_ROWS),
+        )
+        sort_bf = const.tile([P, P], BF16)
+        nc.vector.tensor_copy(
+            out=sort_bf[:].rearrange("i (r b) -> i r b", r=BONE_ROWS),
+            in_=ident_bf[:].rearrange("i (b r) -> i r b", r=BONE_ROWS),
+        )
+
+        h_raws, c_raws, wz_raws, wz_groupeds = {}, {}, {}, {}
+        h_ops, wz_ops, gate_tiles, c_turneds = {}, {}, {}, {}
+
+        def load_rows(raw, src, t):
+            for r in range(BONE_ROWS):
+                nc.sync.dma_start(
+                    out=raw[r:P:BONE_ROWS, :],
+                    in_=src[:, t, r * BONE_STEPS : (r + 1) * BONE_STEPS, :].rearrange("b n k -> b (n k)"),
+                )
+
+        def load_h(t):
+            h_raw = frames.tile([P, BONE_STEPS * FEAT], BF16)
+            load_rows(h_raw, h_new, t)
+            h_raws[t] = h_raw
+
+        def load_c(t):
+            c_raw = frames.tile([P, BONE_STEPS * FEAT], BF16)
+            load_rows(c_raw, c_new, t)
+            c_raws[t] = c_raw
+
+        def load_weights(i):
+            t, g = divmod(i, GATES)
+            wz_raw = raws.tile([P, 2, PACK, FEAT], BF16)
+            for m, weights in enumerate((Wg_s, Zg_s)):
+                nc.sync.dma_start(
+                    out=wz_raw[:, m].rearrange("q j w -> q (j w)"),
+                    in_=weights[g, t].rearrange("(q j) w -> q (j w)", j=PACK),
+                )
+            wz_raws[i] = wz_raw
+
+        def regroup_weights(i, m):
+            if m == 0:
+                wz_grouped = stage.tile([P, 2, FEAT, PACK], BF16, align_bytes=64)
+                wz_groupeds[i] = wz_grouped
+            nc.vector.tensor_copy(
+                out=wz_groupeds[i][:, m].rearrange("q (c i) j -> q c j i", i=4),
+                in_=wz_raws[i][:, m].rearrange("q j (c i) -> q c j i", i=4),
+            )
+
+        def quantise_weights(i):
+            wz_words = weight_ops.tile([P, 2 * FEAT], U32, align_bytes=64)
+            wz_scales = weight_ops.tile([P, 2 * FEAT], U8, align_bytes=64)
+            nc.vector.quantize_mx(
+                out=wz_words[:].bitcast(FP8X4),
+                scales=wz_scales[:],
+                in_=wz_groupeds[i][:].rearrange("q m w j -> q (m w j)"),
+            )
+            wz_ops[i] = (wz_words, wz_scales)
+
+        def turn_frame(t):
+            h_as_words = h_raws[t][:].bitcast(F32)
+            h_grouped = stage.tile([P, COLS * PACK], BF16, align_bytes=64)
+            h_grouped_words = h_grouped[:].bitcast(F32).rearrange("q (n c u) -> q n c u", c=P, u=2)
+            for pair in range(BONE_STEPS // 2):
+                turned = flip.tile([P, 2, 2, P], F32, tag="flip")
+                for a in range(2):
+                    first_word = (2 * pair + a) * WORDS
+                    for u in range(2):
+                        nc.tensor.transpose(
+                            out=turned[:, a, u, :],
+                            in_=h_as_words[:, first_word + u : first_word + WORDS : 2],
+                            identity=sort_f32[:],
+                        )
+                nc.scalar.copy(
+                    out=h_grouped_words[:, 2 * pair : 2 * pair + 2],
+                    in_=turned[:].rearrange("q a u c -> q a c u"),
+                )
+            g_grouped = stage.tile([P, BANK * PACK], BF16, align_bytes=64)
+            nc.scalar.copy(
+                out=g_grouped[:].bitcast(F32).rearrange("q (n b u) -> q n b u", b=SEQS, u=2),
+                in_=g_sorted[:, :, t * SEQS : (t + 1) * SEQS]
+                .rearrange("q u b -> q b u")
+                .unsqueeze(1)
+                .to_broadcast([P, BANK_BONES, SEQS, 2]),
+            )
+            return h_grouped, g_grouped
+
+        def quantise_frame(t, h_grouped, g_grouped):
+            h_words = frame_ops.tile([P, COLS], U32, align_bytes=64)
+            h_scales = frame_ops.tile([P, COLS], U8, align_bytes=64)
+            nc.vector.quantize_mx(out=h_words[:].bitcast(FP8X4), scales=h_scales[:], in_=h_grouped[:])
+            g_words = frame_ops.tile([P, BANK], U32, align_bytes=64)
+            g_scales = frame_ops.tile([P, BANK], U8, align_bytes=64)
+            nc.vector.quantize_mx(out=g_words[:].bitcast(FP8X4), scales=g_scales[:], in_=g_grouped[:])
+            h_ops[t] = (h_words, h_scales, g_words, g_scales)
+
+        def start_gate(i):
+            t, g = divmod(i, GATES)
+            values = gate_pool.tile([P, BONES, FEAT_TILES, SEQS], F32)
+            gate_tiles[i] = values
+            if g == F_GATE:
+                for x in range(FEAT_TILES):
+                    c_turned = flip.tile([P, COLS], BF16, tag="flip")
+                    for n in range(BONE_STEPS):
+                        nc.tensor.transpose(
+                            out=c_turned[:, n * P : (n + 1) * P],
+                            in_=c_raws[t][:, n * FEAT + x * P : n * FEAT + (x + 1) * P],
+                            identity=sort_bf[:],
+                        )
+                    c_turneds[x] = c_turned
+
+        def gate_tile(i, x):
+            t, g = divmod(i, GATES)
+            wz_words, wz_scales = wz_ops[i]
+            h_words, h_scales, g_words, g_scales = h_ops[t]
+            values = gate_tiles[i]
+            w_cols = slice(x * P, (x + 1) * P)
+            z_cols = slice(FEAT + x * P, FEAT + (x + 1) * P)
+            for half in range(HALVES):
+                h_cols = slice(half * BANK, (half + 1) * BANK)
+                pre = mm.tile([P, BANK], F32)
+                nc.tensor.matmul_mx(
+                    out=pre[:],
+                    lhsT=wz_words[:, w_cols].bitcast(FP8X4),
+                    lhsT_scale=wz_scales[:, w_cols],
+                    rhs=h_words[:, h_cols].bitcast(FP8X4),
+                    rhs_scale=h_scales[:, h_cols],
+                    start=True,
+                    stop=False,
+                )
+                nc.tensor.matmul_mx(
+                    out=pre[:],
+                    lhsT=wz_words[:, z_cols].bitcast(FP8X4),
+                    lhsT_scale=wz_scales[:, z_cols],
+                    rhs=g_words[:].bitcast(FP8X4),
+                    rhs_scale=g_scales[:],
+                    start=False,
+                    stop=True,
+                )
+                bias_col = (g * FRAMES + t) * FEAT_TILES + x
+                nc.scalar.activation(
+                    out=values[:, half * BANK_BONES : (half + 1) * BANK_BONES, x, :],
+                    in_=pre[:].rearrange("p (n b) -> p n b", b=SEQS),
+                    func=ACT.Sigmoid,
+                    bias=bias_cols[:, bias_col : bias_col + 1],
+                    scale=1.0,
+                )
+            if g == F_GATE:
+                nc.vector.tensor_tensor(
+                    out=values[:, :, x, :],
+                    in0=values[:, :, x, :],
+                    in1=c_turneds[x][:].rearrange("p (n b) -> p n b", b=SEQS),
+                    op=ALU.mult,
+                )
+
+        def fold_bones(i):
+            values = gate_tiles[i]
+            lower = values[:, 0:BANK_BONES].rearrange("p n x b -> p (n x b)")
+            upper = values[:, BANK_BONES:BONES].rearrange("p n x b -> p (n x b)")
+            nc.vector.tensor_tensor(out=lower, in0=lower, in1=upper, op=ALU.add)
+
+        def sum_bones(i):
+            t, g = divmod(i, GATES)
+            values = gate_tiles[i]
+            total = flip.tile([P, P], F32, tag="flip")
+            for n in range(BANK_BONES):
+                nc.tensor.matmul(
+                    out=total[:],
+                    lhsT=values[:, n].rearrange("p x b -> p (x b)"),
+                    rhs=ident_f32[:],
+                    is_transpose=True,
+                    start=(n == 0),
+                    stop=(n == BANK_BONES - 1),
+                )
+            nc.scalar.mul(out=means[:, g, t, :], in_=total[:], mul=1.0 / BONES)
+            if g == GG_GATE:
+                nc.vector.tensor_tensor(out=c_out[:, t, :], in0=means[:, GG_GATE, t, :], in1=cg[:, t, :], op=ALU.mult)
+                nc.vector.tensor_tensor(out=c_out[:, t, :], in0=c_out[:, t, :], in1=means[:, F_GATE, t, :], op=ALU.add)
+
+        bias_rows = const.tile([P, P], BF16)
+        nc.vector.memset(bias_rows[:], 0.0)
+        g_raw = const.tile([P, FEAT], BF16)
+        nc.sync.dma_start(out=g_raw[:], in_=g_s.rearrange("b t k -> (b t) k"))
+        nc.sync.dma_start(
+            out=bias_rows[0 : UNITS * FEAT_TILES, :],
+            in_=bg_s.rearrange("g t o (x p) -> (g t o x) p", p=P),
+        )
+        load_h(0)
+        load_weights(0)
+        load_c(0)
+        for i in range(1, AHEAD + 1):
+            load_weights(i)
+        cg = const.tile([P, FRAMES, P], BF16)
+        for x in range(FEAT_TILES):
+            nc.sync.dma_start(out=cg[x * SEQS : (x + 1) * SEQS], in_=c_g_s[:, :, x * P : (x + 1) * P])
+
+        g_turned = flip.tile([P, 2, P], F32, tag="flip")
+        for u in range(2):
+            nc.tensor.transpose(
+                out=g_turned[:, u, :],
+                in_=g_raw[:].bitcast(F32)[:, u:WORDS:2],
+                identity=sort_f32[:],
+            )
+        g_sorted = const.tile([P, 2, P], F32)
+        nc.scalar.copy(out=g_sorted[:], in_=g_turned[:])
+        bias_turned = flip.tile([P, P], BF16, tag="flip")
+        nc.tensor.transpose(out=bias_turned[:], in_=bias_rows[:], identity=ident_bf[:])
+        bias_cols = const.tile([P, UNITS * FEAT_TILES], F32)
+        nc.vector.tensor_copy(out=bias_cols[:], in_=bias_turned[:, 0 : UNITS * FEAT_TILES])
+
+        means = const.tile([P, GATES, FRAMES, P], F32)
+        c_out = const.tile([P, FRAMES, P], F32)
+
+        first_h_grouped, first_g_grouped = turn_frame(0)
+        regroup_weights(0, 0)
+        regroup_weights(0, 1)
+        quantise_frame(0, first_h_grouped, first_g_grouped)
+        quantise_weights(0)
+        for i in range(1, AHEAD):
+            regroup_weights(i, 0)
+            regroup_weights(i, 1)
+            quantise_weights(i)
+
+        for i in range(UNITS):
+            t, g = divmod(i, GATES)
+            if g == F_GATE and t + 1 < FRAMES:
+                load_h(t + 1)
+                load_c(t + 1)
+            if i + AHEAD + 1 < UNITS:
+                load_weights(i + AHEAD + 1)
+            start_gate(i)
+            if i + AHEAD < UNITS:
+                regroup_weights(i + AHEAD, 0)
+            for x in range(FEAT_TILES):
+                gate_tile(i, x)
+                if i + AHEAD < UNITS and x == 0:
+                    regroup_weights(i + AHEAD, 1)
+                if i >= 1 and x == 1:
+                    fold_bones(i - 1)
+                if i + AHEAD < UNITS and x == 2:
+                    quantise_weights(i + AHEAD)
+            if i >= SUM_LAG:
+                sum_bones(i - SUM_LAG)
+            if g == GG_GATE and t + 1 < FRAMES:
+                next_h_grouped, next_g_grouped = turn_frame(t + 1)
+                quantise_frame(t + 1, next_h_grouped, next_g_grouped)
+        fold_bones(UNITS - 1)
+        for i in range(UNITS - SUM_LAG, UNITS - 1):
+            sum_bones(i)
+
+        for x in range(FEAT_TILES):
+            nc.sync.dma_start(out=out_1[:, :, x * P : (x + 1) * P], in_=c_out[x * SEQS : (x + 1) * SEQS])
+        tanh_c = const.tile([P, FRAMES, P], F32)
+        nc.scalar.activation(out=tanh_c[:], in_=c_out[:], func=ACT.Tanh)
+        sum_bones(UNITS - 1)
+        g_out = const.tile([P, FRAMES, P], F32)
+        for t in range(FRAMES):
+            nc.vector.tensor_tensor(out=g_out[:, t, :], in0=means[:, O_GATE, t, :], in1=tanh_c[:, t, :], op=ALU.mult)
+        for x in range(FEAT_TILES):
+            nc.sync.dma_start(out=out_0[:, :, x * P : (x + 1) * P], in_=g_out[x * SEQS : (x + 1) * SEQS])

@@ -28,8 +28,11 @@ COLS = BONES * SEQS
 BANK = 512
 HALVES = COLS // BANK
 BANK_BONES = BANK // SEQS
+HALF_STEPS = BONE_STEPS // HALVES
 AHEAD = 2
 SUM_LAG = 2
+Z_ON_SCALAR = (F_GATE,)
+LAST_SPLIT = 2
 
 FLOPS = 2 * GATES * FRAMES * FEAT * FEAT * (COLS + SEQS)
 
@@ -48,6 +51,9 @@ def tile_st_hmr_pc_t_kernel(tc, h_new, c_new, g_s, c_g_s, Wg_s, Zg_s, bg_s, out_
         flip = ctx.enter_context(tc.psum_pool(name="flip", bufs=4))
         ctx.enter_context(tc.manual_schedule())
 
+        warm = const.tile([P, 2], F32)
+        nc.vector.memset(warm[:], 0.0)
+        nc.scalar.activation(out=warm[:, 1:2], in_=warm[:, 0:1], func=ACT.Sigmoid)
         ident_f32 = const.tile([P, P], F32)
         make_identity(nc, ident_f32[:])
         ident_bf = const.tile([P, P], BF16)
@@ -62,42 +68,45 @@ def tile_st_hmr_pc_t_kernel(tc, h_new, c_new, g_s, c_g_s, Wg_s, Zg_s, bg_s, out_
             out=sort_bf[:].rearrange("i (r b) -> i r b", r=BONE_ROWS),
             in_=ident_bf[:].rearrange("i (b r) -> i r b", r=BONE_ROWS),
         )
+        bias_rows = const.tile([P, P], BF16)
+        nc.vector.memset(bias_rows[:], 0.0)
 
         h_raws, c_raws, wz_raws, wz_groupeds = {}, {}, {}, {}
-        h_ops, wz_ops, gate_tiles, c_turneds = {}, {}, {}, {}
+        h_ops, g_ops, wz_ops, gate_tiles, c_turneds, totals = {}, {}, {}, {}, {}, {}
 
-        def load_rows(raw, src, t):
+        def load_rows(raw, src, t, first_step, end_step):
             for r in range(BONE_ROWS):
                 nc.sync.dma_start(
                     out=raw[r:P:BONE_ROWS, :],
-                    in_=src[:, t, r * BONE_STEPS : (r + 1) * BONE_STEPS, :].rearrange("b n k -> b (n k)"),
+                    in_=src[:, t, r * BONE_STEPS + first_step : r * BONE_STEPS + end_step, :].rearrange("b n k -> b (n k)"),
                 )
 
-        def load_h(t):
-            h_raw = frames.tile([P, BONE_STEPS * FEAT], BF16)
-            load_rows(h_raw, h_new, t)
-            h_raws[t] = h_raw
+        def load_h(t, half):
+            h_raw = frames.tile([P, HALF_STEPS * FEAT], BF16, bufs=2 * HALVES)
+            load_rows(h_raw, h_new, t, half * HALF_STEPS, (half + 1) * HALF_STEPS)
+            h_raws[t, half] = h_raw
 
         def load_c(t):
             c_raw = frames.tile([P, BONE_STEPS * FEAT], BF16)
-            load_rows(c_raw, c_new, t)
+            load_rows(c_raw, c_new, t, 0, BONE_STEPS)
             c_raws[t] = c_raw
 
-        def load_weights(i):
+        def load_weights(i, matrices):
             t, g = divmod(i, GATES)
-            wz_raw = raws.tile([P, 2, PACK, FEAT], BF16)
-            for m, weights in enumerate((Wg_s, Zg_s)):
+            if i not in wz_raws:
+                wz_raw = raws.tile([P, 2, PACK, FEAT], BF16)
+                wz_raws[i] = wz_raw
+            for m in matrices:
                 nc.sync.dma_start(
-                    out=wz_raw[:, m].rearrange("q j w -> q (j w)"),
-                    in_=weights[g, t].rearrange("(q j) w -> q (j w)", j=PACK),
+                    out=wz_raws[i][:, m].rearrange("q j w -> q (j w)"),
+                    in_=(Wg_s, Zg_s)[m][g, t].rearrange("(q j) w -> q (j w)", j=PACK),
                 )
-            wz_raws[i] = wz_raw
 
-        def regroup_weights(i, m):
-            if m == 0:
+        def regroup_weights(i, m, copy):
+            if i not in wz_groupeds:
                 wz_grouped = stage.tile([P, 2, FEAT, PACK], BF16, align_bytes=64)
                 wz_groupeds[i] = wz_grouped
-            nc.vector.tensor_copy(
+            copy(
                 out=wz_groupeds[i][:, m].rearrange("q (c i) j -> q c j i", i=4),
                 in_=wz_raws[i][:, m].rearrange("q j (c i) -> q c j i", i=4),
             )
@@ -112,11 +121,14 @@ def tile_st_hmr_pc_t_kernel(tc, h_new, c_new, g_s, c_g_s, Wg_s, Zg_s, bg_s, out_
             )
             wz_ops[i] = (wz_words, wz_scales)
 
-        def turn_frame(t):
-            h_as_words = h_raws[t][:].bitcast(F32)
+        def new_h_grouped():
             h_grouped = stage.tile([P, COLS * PACK], BF16, align_bytes=64)
+            return h_grouped
+
+        def turn_half(t, half, h_grouped):
+            h_as_words = h_raws[t, half][:].bitcast(F32)
             h_grouped_words = h_grouped[:].bitcast(F32).rearrange("q (n c u) -> q n c u", c=P, u=2)
-            for pair in range(BONE_STEPS // 2):
+            for pair in range(HALF_STEPS // 2):
                 turned = flip.tile([P, 2, 2, P], F32, tag="flip")
                 for a in range(2):
                     first_word = (2 * pair + a) * WORDS
@@ -126,10 +138,13 @@ def tile_st_hmr_pc_t_kernel(tc, h_new, c_new, g_s, c_g_s, Wg_s, Zg_s, bg_s, out_
                             in_=h_as_words[:, first_word + u : first_word + WORDS : 2],
                             identity=sort_f32[:],
                         )
+                step = half * HALF_STEPS + 2 * pair
                 nc.scalar.copy(
-                    out=h_grouped_words[:, 2 * pair : 2 * pair + 2],
+                    out=h_grouped_words[:, step : step + 2],
                     in_=turned[:].rearrange("q a u c -> q a c u"),
                 )
+
+        def repeat_g(t):
             g_grouped = stage.tile([P, BANK * PACK], BF16, align_bytes=64)
             nc.scalar.copy(
                 out=g_grouped[:].bitcast(F32).rearrange("q (n b u) -> q n b u", b=SEQS, u=2),
@@ -138,75 +153,103 @@ def tile_st_hmr_pc_t_kernel(tc, h_new, c_new, g_s, c_g_s, Wg_s, Zg_s, bg_s, out_
                 .unsqueeze(1)
                 .to_broadcast([P, BANK_BONES, SEQS, 2]),
             )
-            return h_grouped, g_grouped
+            return g_grouped
 
-        def quantise_frame(t, h_grouped, g_grouped):
-            h_words = frame_ops.tile([P, COLS], U32, align_bytes=64)
-            h_scales = frame_ops.tile([P, COLS], U8, align_bytes=64)
-            nc.vector.quantize_mx(out=h_words[:].bitcast(FP8X4), scales=h_scales[:], in_=h_grouped[:])
+        def quantise_h(t, h_grouped, half):
+            if t not in h_ops:
+                h_words = frame_ops.tile([P, COLS], U32, align_bytes=64)
+                h_scales = frame_ops.tile([P, COLS], U8, align_bytes=64)
+                h_ops[t] = (h_words, h_scales)
+            words, scales = h_ops[t]
+            cols = slice(half * BANK, (half + 1) * BANK)
+            nc.vector.quantize_mx(
+                out=words[:, cols].bitcast(FP8X4),
+                scales=scales[:, cols],
+                in_=h_grouped[:, half * BANK * PACK : (half + 1) * BANK * PACK],
+            )
+
+        def quantise_g(t, g_grouped):
             g_words = frame_ops.tile([P, BANK], U32, align_bytes=64)
             g_scales = frame_ops.tile([P, BANK], U8, align_bytes=64)
             nc.vector.quantize_mx(out=g_words[:].bitcast(FP8X4), scales=g_scales[:], in_=g_grouped[:])
-            h_ops[t] = (h_words, h_scales, g_words, g_scales)
+            g_ops[t] = (g_words, g_scales)
 
-        def start_gate(i):
-            t, g = divmod(i, GATES)
+        def turn_c(t):
+            for x in range(FEAT_TILES):
+                c_turned = flip.tile([P, COLS], BF16, tag="flip")
+                for n in range(BONE_STEPS):
+                    nc.tensor.transpose(
+                        out=c_turned[:, n * P : (n + 1) * P],
+                        in_=c_raws[t][:, n * FEAT + x * P : n * FEAT + (x + 1) * P],
+                        identity=sort_bf[:],
+                    )
+                c_turneds[x] = c_turned
+
+        def new_values(i):
             values = gate_pool.tile([P, BONES, FEAT_TILES, SEQS], F32)
             gate_tiles[i] = values
-            if g == F_GATE:
-                for x in range(FEAT_TILES):
-                    c_turned = flip.tile([P, COLS], BF16, tag="flip")
-                    for n in range(BONE_STEPS):
-                        nc.tensor.transpose(
-                            out=c_turned[:, n * P : (n + 1) * P],
-                            in_=c_raws[t][:, n * FEAT + x * P : n * FEAT + (x + 1) * P],
-                            identity=sort_bf[:],
-                        )
-                    c_turneds[x] = c_turned
 
-        def gate_tile(i, x):
-            t, g = divmod(i, GATES)
+        def multiply(i, x, half):
             wz_words, wz_scales = wz_ops[i]
-            h_words, h_scales, g_words, g_scales = h_ops[t]
-            values = gate_tiles[i]
+            h_words, h_scales = h_ops[i // GATES]
+            g_words, g_scales = g_ops[i // GATES]
             w_cols = slice(x * P, (x + 1) * P)
             z_cols = slice(FEAT + x * P, FEAT + (x + 1) * P)
+            h_cols = slice(half * BANK, (half + 1) * BANK)
+            pre = mm.tile([P, BANK], F32)
+            nc.tensor.matmul_mx(
+                out=pre[:],
+                lhsT=wz_words[:, w_cols].bitcast(FP8X4),
+                lhsT_scale=wz_scales[:, w_cols],
+                rhs=h_words[:, h_cols].bitcast(FP8X4),
+                rhs_scale=h_scales[:, h_cols],
+                start=True,
+                stop=False,
+            )
+            nc.tensor.matmul_mx(
+                out=pre[:],
+                lhsT=wz_words[:, z_cols].bitcast(FP8X4),
+                lhsT_scale=wz_scales[:, z_cols],
+                rhs=g_words[:].bitcast(FP8X4),
+                rhs_scale=g_scales[:],
+                start=False,
+                stop=True,
+            )
+            return pre
+
+        def squash(i, x, half, pre, bones):
+            t, g = divmod(i, GATES)
+            bias_col = (g * FRAMES + t) * FEAT_TILES + x
+            nc.scalar.activation(
+                out=gate_tiles[i][:, half * BANK_BONES + bones.start : half * BANK_BONES + bones.stop, x, :],
+                in_=pre[:].rearrange("p (n b) -> p n b", b=SEQS)[:, bones],
+                func=ACT.Sigmoid,
+                bias=bias_cols[:, bias_col : bias_col + 1],
+                scale=1.0,
+            )
+
+        def gate_tile(i, x):
             for half in range(HALVES):
-                h_cols = slice(half * BANK, (half + 1) * BANK)
-                pre = mm.tile([P, BANK], F32)
-                nc.tensor.matmul_mx(
-                    out=pre[:],
-                    lhsT=wz_words[:, w_cols].bitcast(FP8X4),
-                    lhsT_scale=wz_scales[:, w_cols],
-                    rhs=h_words[:, h_cols].bitcast(FP8X4),
-                    rhs_scale=h_scales[:, h_cols],
-                    start=True,
-                    stop=False,
-                )
-                nc.tensor.matmul_mx(
-                    out=pre[:],
-                    lhsT=wz_words[:, z_cols].bitcast(FP8X4),
-                    lhsT_scale=wz_scales[:, z_cols],
-                    rhs=g_words[:].bitcast(FP8X4),
-                    rhs_scale=g_scales[:],
-                    start=False,
-                    stop=True,
-                )
-                bias_col = (g * FRAMES + t) * FEAT_TILES + x
-                nc.scalar.activation(
-                    out=values[:, half * BANK_BONES : (half + 1) * BANK_BONES, x, :],
-                    in_=pre[:].rearrange("p (n b) -> p n b", b=SEQS),
-                    func=ACT.Sigmoid,
-                    bias=bias_cols[:, bias_col : bias_col + 1],
-                    scale=1.0,
-                )
-            if g == F_GATE:
-                nc.vector.tensor_tensor(
-                    out=values[:, :, x, :],
-                    in0=values[:, :, x, :],
-                    in1=c_turneds[x][:].rearrange("p (n b) -> p n b", b=SEQS),
-                    op=ALU.mult,
-                )
+                pre = multiply(i, x, half)
+                squash(i, x, half, pre, slice(0, BANK_BONES))
+
+        def weigh_by_c(i, x):
+            values = gate_tiles[i]
+            nc.vector.tensor_tensor(
+                out=values[:, :, x, :],
+                in0=values[:, :, x, :],
+                in1=c_turneds[x][:].rearrange("p (n b) -> p n b", b=SEQS),
+                op=ALU.mult,
+            )
+
+        def fold_tile(i, x):
+            values = gate_tiles[i]
+            nc.gpsimd.tensor_tensor(
+                out=values[:, 0:BANK_BONES, x, :],
+                in0=values[:, 0:BANK_BONES, x, :],
+                in1=values[:, BANK_BONES:BONES, x, :],
+                op=ALU.add,
+            )
 
         def fold_bones(i):
             values = gate_tiles[i]
@@ -214,41 +257,64 @@ def tile_st_hmr_pc_t_kernel(tc, h_new, c_new, g_s, c_g_s, Wg_s, Zg_s, bg_s, out_
             upper = values[:, BANK_BONES:BONES].rearrange("p n x b -> p (n x b)")
             nc.vector.tensor_tensor(out=lower, in0=lower, in1=upper, op=ALU.add)
 
-        def sum_bones(i):
-            t, g = divmod(i, GATES)
-            values = gate_tiles[i]
-            total = flip.tile([P, P], F32, tag="flip")
-            for n in range(BANK_BONES):
+        def sum_bones(i, bones, first, last):
+            if first:
+                total = flip.tile([P, P], F32, tag="flip")
+                totals[i] = total
+            for n in bones:
                 nc.tensor.matmul(
-                    out=total[:],
-                    lhsT=values[:, n].rearrange("p x b -> p (x b)"),
+                    out=totals[i][:],
+                    lhsT=gate_tiles[i][:, n].rearrange("p x b -> p (x b)"),
                     rhs=ident_f32[:],
                     is_transpose=True,
-                    start=(n == 0),
-                    stop=(n == BANK_BONES - 1),
+                    start=(first and n == bones[0]),
+                    stop=(last and n == bones[-1]),
                 )
-            nc.scalar.mul(out=means[:, g, t, :], in_=total[:], mul=1.0 / BONES)
-            if g == GG_GATE:
-                nc.vector.tensor_tensor(out=c_out[:, t, :], in0=means[:, GG_GATE, t, :], in1=cg[:, t, :], op=ALU.mult)
-                nc.vector.tensor_tensor(out=c_out[:, t, :], in0=c_out[:, t, :], in1=means[:, F_GATE, t, :], op=ALU.add)
 
-        bias_rows = const.tile([P, P], BF16)
-        nc.vector.memset(bias_rows[:], 0.0)
+        def finish(i):
+            t, g = divmod(i, GATES)
+            if g == O_GATE:
+                nc.vector.scalar_tensor_tensor(
+                    out=g_out[:, t, :], in0=totals[i][:], scalar=1.0 / BONES, in1=tanh_c[:, t, :],
+                    op0=ALU.mult, op1=ALU.mult,
+                )
+            else:
+                nc.scalar.mul(out=means[:, g, t, :], in_=totals[i][:], mul=1.0 / BONES)
+
+        def combine(t):
+            nc.vector.tensor_tensor(out=c_out[:, t, :], in0=means[:, GG_GATE, t, :], in1=cg[:, t, :], op=ALU.mult)
+            nc.vector.tensor_tensor(out=c_out[:, t, :], in0=c_out[:, t, :], in1=means[:, F_GATE, t, :], op=ALU.add)
+
+        def store(dram, tile, first_t, end_t):
+            for x in range(FEAT_TILES):
+                nc.sync.dma_start(
+                    out=dram[:, first_t:end_t, x * P : (x + 1) * P], in_=tile[x * SEQS : (x + 1) * SEQS, first_t:end_t]
+                )
+
         g_raw = const.tile([P, FEAT], BF16)
+        cg = const.tile([P, FRAMES, P], BF16)
+        load_h(0, 0)
+        load_weights(0, [0])
         nc.sync.dma_start(out=g_raw[:], in_=g_s.rearrange("b t k -> (b t) k"))
         nc.sync.dma_start(
             out=bias_rows[0 : UNITS * FEAT_TILES, :],
             in_=bg_s.rearrange("g t o (x p) -> (g t o x) p", p=P),
         )
-        load_h(0)
-        load_weights(0)
+        load_h(0, 1)
+        load_weights(0, [1])
         load_c(0)
         for i in range(1, AHEAD + 1):
-            load_weights(i)
-        cg = const.tile([P, FRAMES, P], BF16)
+            load_weights(i, range(2))
         for x in range(FEAT_TILES):
             nc.sync.dma_start(out=cg[x * SEQS : (x + 1) * SEQS], in_=c_g_s[:, :, x * P : (x + 1) * P])
 
+        means = const.tile([P, O_GATE, FRAMES, P], F32)
+        c_out = const.tile([P, FRAMES, P], F32)
+        tanh_c = const.tile([P, FRAMES, P], F32)
+        g_out = const.tile([P, FRAMES, P], F32)
+
+        h_grouped = new_h_grouped()
+        turn_half(0, 0, h_grouped)
         g_turned = flip.tile([P, 2, P], F32, tag="flip")
         for u in range(2):
             nc.tensor.transpose(
@@ -258,58 +324,89 @@ def tile_st_hmr_pc_t_kernel(tc, h_new, c_new, g_s, c_g_s, Wg_s, Zg_s, bg_s, out_
             )
         g_sorted = const.tile([P, 2, P], F32)
         nc.scalar.copy(out=g_sorted[:], in_=g_turned[:])
+        g_grouped = repeat_g(0)
         bias_turned = flip.tile([P, P], BF16, tag="flip")
         nc.tensor.transpose(out=bias_turned[:], in_=bias_rows[:], identity=ident_bf[:])
         bias_cols = const.tile([P, UNITS * FEAT_TILES], F32)
+        turn_half(0, 1, h_grouped)
+
+        regroup_weights(0, 0, nc.vector.tensor_copy)
+        quantise_h(0, h_grouped, 0)
         nc.vector.tensor_copy(out=bias_cols[:], in_=bias_turned[:, 0 : UNITS * FEAT_TILES])
-
-        means = const.tile([P, GATES, FRAMES, P], F32)
-        c_out = const.tile([P, FRAMES, P], F32)
-
-        first_h_grouped, first_g_grouped = turn_frame(0)
-        regroup_weights(0, 0)
-        regroup_weights(0, 1)
-        quantise_frame(0, first_h_grouped, first_g_grouped)
+        quantise_g(0, g_grouped)
+        regroup_weights(0, 1, nc.vector.tensor_copy)
         quantise_weights(0)
-        for i in range(1, AHEAD):
-            regroup_weights(i, 0)
-            regroup_weights(i, 1)
-            quantise_weights(i)
+        quantise_h(0, h_grouped, 1)
+        for m in range(2):
+            regroup_weights(1, m, nc.vector.tensor_copy)
 
-        for i in range(UNITS):
+        for i in range(UNITS - 1):
             t, g = divmod(i, GATES)
             if g == F_GATE and t + 1 < FRAMES:
-                load_h(t + 1)
+                for half in range(HALVES):
+                    load_h(t + 1, half)
                 load_c(t + 1)
             if i + AHEAD + 1 < UNITS:
-                load_weights(i + AHEAD + 1)
-            start_gate(i)
-            if i + AHEAD < UNITS:
-                regroup_weights(i + AHEAD, 0)
-            for x in range(FEAT_TILES):
-                gate_tile(i, x)
-                if i + AHEAD < UNITS and x == 0:
-                    regroup_weights(i + AHEAD, 1)
-                if i >= 1 and x == 1:
-                    fold_bones(i - 1)
-                if i + AHEAD < UNITS and x == 2:
-                    quantise_weights(i + AHEAD)
-            if i >= SUM_LAG:
-                sum_bones(i - SUM_LAG)
-            if g == GG_GATE and t + 1 < FRAMES:
-                next_h_grouped, next_g_grouped = turn_frame(t + 1)
-                quantise_frame(t + 1, next_h_grouped, next_g_grouped)
-        fold_bones(UNITS - 1)
-        for i in range(UNITS - SUM_LAG, UNITS - 1):
-            sum_bones(i)
+                load_weights(i + AHEAD + 1, range(2))
 
-        for x in range(FEAT_TILES):
-            nc.sync.dma_start(out=out_1[:, :, x * P : (x + 1) * P], in_=c_out[x * SEQS : (x + 1) * SEQS])
-        tanh_c = const.tile([P, FRAMES, P], F32)
-        nc.scalar.activation(out=tanh_c[:], in_=c_out[:], func=ACT.Tanh)
-        sum_bones(UNITS - 1)
-        g_out = const.tile([P, FRAMES, P], F32)
-        for t in range(FRAMES):
-            nc.vector.tensor_tensor(out=g_out[:, t, :], in0=means[:, O_GATE, t, :], in1=tanh_c[:, t, :], op=ALU.mult)
-        for x in range(FEAT_TILES):
-            nc.sync.dma_start(out=out_0[:, :, x * P : (x + 1) * P], in_=g_out[x * SEQS : (x + 1) * SEQS])
+            quantise_weights(i + 1)
+            if g == O_GATE:
+                h_grouped = new_h_grouped()
+                for half in range(HALVES):
+                    turn_half(t + 1, half, h_grouped)
+                g_grouped = repeat_g(t + 1)
+            if i >= SUM_LAG:
+                sum_bones(i - SUM_LAG, range(BANK_BONES), True, True)
+                finish(i - SUM_LAG)
+            if i + AHEAD < UNITS:
+                regroup_weights(i + AHEAD, 0, nc.vector.tensor_copy)
+                if g in Z_ON_SCALAR and i > 0:
+                    regroup_weights(i + AHEAD, 1, nc.scalar.copy)
+                else:
+                    regroup_weights(i + AHEAD, 1, nc.vector.tensor_copy)
+            if i >= 1 and (i - 1) % GATES != F_GATE:
+                fold_bones(i - 1)
+            if g == F_GATE and t >= 1:
+                combine(t - 1)
+            if g == O_GATE:
+                for half in range(HALVES):
+                    quantise_h(t + 1, h_grouped, half)
+                quantise_g(t + 1, g_grouped)
+            new_values(i)
+            first_tiles = 2 if i == 0 else 0
+            for x in range(first_tiles):
+                gate_tile(i, x)
+            if g == F_GATE:
+                turn_c(t)
+            for x in range(first_tiles, FEAT_TILES):
+                gate_tile(i, x)
+            if g == F_GATE:
+                for x in range(FEAT_TILES):
+                    weigh_by_c(i, x)
+                    fold_tile(i, x)
+                if t >= 1:
+                    nc.scalar.activation(out=tanh_c[:, t - 1, :], in_=c_out[:, t - 1, :], func=ACT.Tanh)
+
+        i = UNITS - 1
+        t = FRAMES - 1
+        fold_bones(i - 1)
+        sum_bones(i - SUM_LAG, range(BANK_BONES), True, True)
+        finish(i - SUM_LAG)
+        store(out_0, g_out, 0, t)
+        new_values(i)
+        for half in range(HALVES):
+            pres = [multiply(i, x, half) for x in range(FEAT_TILES)]
+            pieces = LAST_SPLIT if half == HALVES - 1 else 1
+            step = BANK_BONES // pieces
+            for piece in range(pieces):
+                for x in range(FEAT_TILES):
+                    squash(i, x, half, pres[x], slice(piece * step, (piece + 1) * step))
+            if half == 0:
+                sum_bones(i - 1, range(BANK_BONES), True, True)
+                finish(i - 1)
+                combine(t)
+        nc.scalar.activation(out=tanh_c[:, t, :], in_=c_out[:, t, :], func=ACT.Tanh)
+        store(out_1, c_out, 0, FRAMES)
+        sum_bones(i, range(BONES), True, True)
+        finish(i)
+        store(out_0, g_out, t, FRAMES)

@@ -242,15 +242,6 @@ def tile_st_hmr_pc_t_kernel(tc, h_new, c_new, g_s, c_g_s, Wg_s, Zg_s, bg_s, out_
                 op=ALU.mult,
             )
 
-        def fold_tile(i, x):
-            values = gate_tiles[i]
-            nc.gpsimd.tensor_tensor(
-                out=values[:, 0:BANK_BONES, x, :],
-                in0=values[:, 0:BANK_BONES, x, :],
-                in1=values[:, BANK_BONES:BONES, x, :],
-                op=ALU.add,
-            )
-
         def fold_bones(i):
             values = gate_tiles[i]
             lower = values[:, 0:BANK_BONES].rearrange("p n x b -> p (n x b)")
@@ -364,7 +355,7 @@ def tile_st_hmr_pc_t_kernel(tc, h_new, c_new, g_s, c_g_s, Wg_s, Zg_s, bg_s, out_
                     regroup_weights(i + AHEAD, 1, nc.scalar.copy)
                 else:
                     regroup_weights(i + AHEAD, 1, nc.vector.tensor_copy)
-            if i >= 1 and (i - 1) % GATES != F_GATE:
+            if i >= 1:
                 fold_bones(i - 1)
             if g == F_GATE and t >= 1:
                 combine(t - 1)
@@ -383,7 +374,6 @@ def tile_st_hmr_pc_t_kernel(tc, h_new, c_new, g_s, c_g_s, Wg_s, Zg_s, bg_s, out_
             if g == F_GATE:
                 for x in range(FEAT_TILES):
                     weigh_by_c(i, x)
-                    fold_tile(i, x)
                 if t >= 1:
                     nc.scalar.activation(out=tanh_c[:, t - 1, :], in_=c_out[:, t - 1, :], func=ACT.Tanh)
 

@@ -19,6 +19,7 @@ BONES = 32
 FEAT = 512
 GATES = 3
 F_GATE, GG_GATE, O_GATE = 0, 1, 2
+W_SIDE, Z_SIDE = 0, 1
 UNITS = FRAMES * GATES
 FEAT_TILES = FEAT // P
 BONE_ROWS = P // SEQS
@@ -29,9 +30,9 @@ BANK = 512
 HALVES = COLS // BANK
 BANK_BONES = BANK // SEQS
 HALF_STEPS = BONE_STEPS // HALVES
-AHEAD = 2
 SUM_LAG = 2
-Z_ON_SCALAR = (F_GATE,)
+GROUP = 256
+MM_BANKS = 4
 LAST_SPLIT = 2
 
 FLOPS = 2 * GATES * FRAMES * FEAT * FEAT * (COLS + SEQS)
@@ -42,13 +43,13 @@ def tile_st_hmr_pc_t_kernel(tc, h_new, c_new, g_s, c_g_s, Wg_s, Zg_s, bg_s, out_
     with ExitStack() as ctx:
         const = ctx.enter_context(tc.tile_pool(name="const", bufs=1))
         frames = ctx.enter_context(tc.tile_pool(name="frames", bufs=2))
-        raws = ctx.enter_context(tc.tile_pool(name="raws", bufs=AHEAD + 1))
+        raws = ctx.enter_context(tc.tile_pool(name="raws", bufs=GATES))
         stage = ctx.enter_context(tc.tile_pool(name="stage", bufs=2))
         frame_ops = ctx.enter_context(tc.tile_pool(name="frame_ops", bufs=2))
-        weight_ops = ctx.enter_context(tc.tile_pool(name="weight_ops", bufs=AHEAD + 1))
+        weight_ops = ctx.enter_context(tc.tile_pool(name="weight_ops", bufs=GATES + 1))
         gate_pool = ctx.enter_context(tc.tile_pool(name="gate_pool", bufs=SUM_LAG + 2))
-        mm = ctx.enter_context(tc.psum_pool(name="mm", bufs=4))
-        flip = ctx.enter_context(tc.psum_pool(name="flip", bufs=4))
+        mm = ctx.enter_context(tc.psum_pool(name="mm", bufs=MM_BANKS))
+        flip = ctx.enter_context(tc.psum_pool(name="flip", bufs=8 - MM_BANKS))
         ctx.enter_context(tc.manual_schedule())
 
         warm = const.tile([P, 2], F32)
@@ -91,24 +92,24 @@ def tile_st_hmr_pc_t_kernel(tc, h_new, c_new, g_s, c_g_s, Wg_s, Zg_s, bg_s, out_
             load_rows(c_raw, c_new, t, 0, BONE_STEPS)
             c_raws[t] = c_raw
 
-        def load_weights(i, matrices):
+        def load_weights(i, matrices, cols=slice(0, FEAT)):
             t, g = divmod(i, GATES)
             if i not in wz_raws:
                 wz_raw = raws.tile([P, 2, PACK, FEAT], BF16)
                 wz_raws[i] = wz_raw
             for m in matrices:
                 nc.sync.dma_start(
-                    out=wz_raws[i][:, m].rearrange("q j w -> q (j w)"),
-                    in_=(Wg_s, Zg_s)[m][g, t].rearrange("(q j) w -> q (j w)", j=PACK),
+                    out=wz_raws[i][:, m, :, cols],
+                    in_=(Wg_s, Zg_s)[m][g, t].rearrange("(q j) w -> q j w", j=PACK)[:, :, cols],
                 )
 
-        def regroup_weights(i, m, copy):
+        def regroup_weights(i, m, copy, cols=slice(0, FEAT)):
             if i not in wz_groupeds:
                 wz_grouped = stage.tile([P, 2, FEAT, PACK], BF16, align_bytes=64)
                 wz_groupeds[i] = wz_grouped
             copy(
-                out=wz_groupeds[i][:, m].rearrange("q (c i) j -> q c j i", i=4),
-                in_=wz_raws[i][:, m].rearrange("q j (c i) -> q c j i", i=4),
+                out=wz_groupeds[i][:, m, cols].rearrange("q (c i) j -> q c j i", i=4),
+                in_=wz_raws[i][:, m, :, cols].rearrange("q j (c i) -> q c j i", i=4),
             )
 
         def quantise_weights(i):
@@ -120,6 +121,19 @@ def tile_st_hmr_pc_t_kernel(tc, h_new, c_new, g_s, c_g_s, Wg_s, Zg_s, bg_s, out_
                 in_=wz_groupeds[i][:].rearrange("q m w j -> q (m w j)"),
             )
             wz_ops[i] = (wz_words, wz_scales)
+
+        def quantise_part(i, m, cols):
+            if i not in wz_ops:
+                wz_words = weight_ops.tile([P, 2 * FEAT], U32, align_bytes=64)
+                wz_scales = weight_ops.tile([P, 2 * FEAT], U8, align_bytes=64)
+                wz_ops[i] = (wz_words, wz_scales)
+            words, scales = wz_ops[i]
+            op_cols = slice(m * FEAT + cols.start, m * FEAT + cols.stop)
+            nc.vector.quantize_mx(
+                out=words[:, op_cols].bitcast(FP8X4),
+                scales=scales[:, op_cols],
+                in_=wz_groupeds[i][:, m, cols].rearrange("q w j -> q (w j)"),
+            )
 
         def new_h_grouped():
             h_grouped = stage.tile([P, COLS * PACK], BF16, align_bytes=64)
@@ -145,13 +159,13 @@ def tile_st_hmr_pc_t_kernel(tc, h_new, c_new, g_s, c_g_s, Wg_s, Zg_s, bg_s, out_
                 )
 
         def repeat_g(t):
-            g_grouped = stage.tile([P, BANK * PACK], BF16, align_bytes=64)
+            g_grouped = stage.tile([P, GROUP * PACK], BF16, align_bytes=64)
             nc.scalar.copy(
                 out=g_grouped[:].bitcast(F32).rearrange("q (n b u) -> q n b u", b=SEQS, u=2),
                 in_=g_sorted[:, :, t * SEQS : (t + 1) * SEQS]
                 .rearrange("q u b -> q b u")
                 .unsqueeze(1)
-                .to_broadcast([P, BANK_BONES, SEQS, 2]),
+                .to_broadcast([P, GROUP // SEQS, SEQS, 2]),
             )
             return g_grouped
 
@@ -169,19 +183,21 @@ def tile_st_hmr_pc_t_kernel(tc, h_new, c_new, g_s, c_g_s, Wg_s, Zg_s, bg_s, out_
             )
 
         def quantise_g(t, g_grouped):
-            g_words = frame_ops.tile([P, BANK], U32, align_bytes=64)
-            g_scales = frame_ops.tile([P, BANK], U8, align_bytes=64)
+            g_words = frame_ops.tile([P, GROUP], U32, align_bytes=64)
+            g_scales = frame_ops.tile([P, GROUP], U8, align_bytes=64)
             nc.vector.quantize_mx(out=g_words[:].bitcast(FP8X4), scales=g_scales[:], in_=g_grouped[:])
             g_ops[t] = (g_words, g_scales)
 
-        def turn_c(t):
-            for x in range(FEAT_TILES):
+        def turn_c(t, tiles):
+            for x in tiles:
                 c_turned = flip.tile([P, COLS], BF16, tag="flip")
                 for n in range(BONE_STEPS):
-                    nc.tensor.transpose(
+                    nc.tensor.matmul(
                         out=c_turned[:, n * P : (n + 1) * P],
-                        in_=c_raws[t][:, n * FEAT + x * P : n * FEAT + (x + 1) * P],
-                        identity=sort_bf[:],
+                        lhsT=c_raws[t][:, n * FEAT + x * P : n * FEAT + (x + 1) * P],
+                        rhs=sort_bf[:],
+                        start=True,
+                        stop=True,
                     )
                 c_turneds[x] = c_turned
 
@@ -189,32 +205,36 @@ def tile_st_hmr_pc_t_kernel(tc, h_new, c_new, g_s, c_g_s, Wg_s, Zg_s, bg_s, out_
             values = gate_pool.tile([P, BONES, FEAT_TILES, SEQS], F32)
             gate_tiles[i] = values
 
-        def multiply(i, x, half):
+        def multiply(i, x, half, late=False):
             wz_words, wz_scales = wz_ops[i]
             h_words, h_scales = h_ops[i // GATES]
             g_words, g_scales = g_ops[i // GATES]
             w_cols = slice(x * P, (x + 1) * P)
             z_cols = slice(FEAT + x * P, FEAT + (x + 1) * P)
-            h_cols = slice(half * BANK, (half + 1) * BANK)
-            pre = mm.tile([P, BANK], F32)
-            nc.tensor.matmul_mx(
-                out=pre[:],
-                lhsT=wz_words[:, w_cols].bitcast(FP8X4),
-                lhsT_scale=wz_scales[:, w_cols],
-                rhs=h_words[:, h_cols].bitcast(FP8X4),
-                rhs_scale=h_scales[:, h_cols],
-                start=True,
-                stop=False,
-            )
-            nc.tensor.matmul_mx(
-                out=pre[:],
-                lhsT=wz_words[:, z_cols].bitcast(FP8X4),
-                lhsT_scale=wz_scales[:, z_cols],
-                rhs=g_words[:].bitcast(FP8X4),
-                rhs_scale=g_scales[:],
-                start=False,
-                stop=True,
-            )
+            if late:
+                pre = flip.tile([P, BANK], F32, tag="flip")
+            else:
+                pre = mm.tile([P, BANK], F32)
+            for first in range(0, BANK, GROUP):
+                cols = slice(half * BANK + first, half * BANK + first + GROUP)
+                nc.tensor.matmul_mx(
+                    out=pre[:, first : first + GROUP],
+                    lhsT=wz_words[:, w_cols].bitcast(FP8X4),
+                    lhsT_scale=wz_scales[:, w_cols],
+                    rhs=h_words[:, cols].bitcast(FP8X4),
+                    rhs_scale=h_scales[:, cols],
+                    start=True,
+                    stop=False,
+                )
+                nc.tensor.matmul_mx(
+                    out=pre[:, first : first + GROUP],
+                    lhsT=wz_words[:, z_cols].bitcast(FP8X4),
+                    lhsT_scale=wz_scales[:, z_cols],
+                    rhs=g_words[:].bitcast(FP8X4),
+                    rhs_scale=g_scales[:],
+                    start=False,
+                    stop=True,
+                )
             return pre
 
         def squash(i, x, half, pre, bones):
@@ -238,7 +258,7 @@ def tile_st_hmr_pc_t_kernel(tc, h_new, c_new, g_s, c_g_s, Wg_s, Zg_s, bg_s, out_
             nc.vector.tensor_tensor(
                 out=values[:, :, x, :],
                 in0=values[:, :, x, :],
-                in1=c_turneds[x][:].rearrange("p (n b) -> p n b", b=SEQS),
+                in1=c_turneds.pop(x)[:].rearrange("p (n b) -> p n b", b=SEQS),
                 op=ALU.mult,
             )
 
@@ -284,17 +304,18 @@ def tile_st_hmr_pc_t_kernel(tc, h_new, c_new, g_s, c_g_s, Wg_s, Zg_s, bg_s, out_
 
         g_raw = const.tile([P, FEAT], BF16)
         cg = const.tile([P, FRAMES, P], BF16)
+        early, late = slice(0, FEAT // 2), slice(FEAT // 2, FEAT)
         load_h(0, 0)
-        load_weights(0, [0])
+        load_weights(0, range(2), early)
         nc.sync.dma_start(out=g_raw[:], in_=g_s.rearrange("b t k -> (b t) k"))
         nc.sync.dma_start(
             out=bias_rows[0 : UNITS * FEAT_TILES, :],
             in_=bg_s.rearrange("g t o (x p) -> (g t o x) p", p=P),
         )
         load_h(0, 1)
-        load_weights(0, [1])
+        load_weights(0, range(2), late)
         load_c(0)
-        for i in range(1, AHEAD + 1):
+        for i in range(1, GATES):
             load_weights(i, range(2))
         for x in range(FEAT_TILES):
             nc.sync.dma_start(out=cg[x * SEQS : (x + 1) * SEQS], in_=c_g_s[:, :, x * P : (x + 1) * P])
@@ -321,15 +342,98 @@ def tile_st_hmr_pc_t_kernel(tc, h_new, c_new, g_s, c_g_s, Wg_s, Zg_s, bg_s, out_
         bias_cols = const.tile([P, UNITS * FEAT_TILES], F32)
         turn_half(0, 1, h_grouped)
 
-        regroup_weights(0, 0, nc.vector.tensor_copy)
+        for m in range(2):
+            regroup_weights(0, m, nc.vector.tensor_copy, early)
+        for m in range(2):
+            quantise_part(0, m, early)
         quantise_h(0, h_grouped, 0)
         nc.vector.tensor_copy(out=bias_cols[:], in_=bias_turned[:, 0 : UNITS * FEAT_TILES])
         quantise_g(0, g_grouped)
-        regroup_weights(0, 1, nc.vector.tensor_copy)
-        quantise_weights(0)
         quantise_h(0, h_grouped, 1)
         for m in range(2):
-            regroup_weights(1, m, nc.vector.tensor_copy)
+            regroup_weights(0, m, nc.vector.tensor_copy, late)
+        for m in range(2):
+            quantise_part(0, m, late)
+        def leave(i):
+            if i >= 0:
+                sum_bones(i, range(BANK_BONES), True, True)
+                finish(i)
+
+        def weigh(i, tiles):
+            for x in tiles:
+                weigh_by_c(i, x)
+
+        def regroup(i, m, copy=nc.vector.tensor_copy):
+            if i < UNITS:
+                regroup_weights(i, m, copy)
+
+        def first_unit():
+            regroup(1, W_SIDE)
+            regroup(1, Z_SIDE)
+            gate_tile(0, 0)
+            turn_c(0, (0, 1))
+            gate_tile(0, 1)
+            weigh(0, (0, 1))
+            turn_c(0, (2, 3))
+            quantise_weights(1)
+            gate_tile(0, 2)
+            regroup(2, W_SIDE)
+            gate_tile(0, 3)
+            weigh(0, (2, 3))
+            regroup(2, Z_SIDE, nc.scalar.copy)
+
+        def f_unit(i):
+            t = i // GATES
+            turn_c(t, (0, 1))
+            fold_bones(i - 1)
+            gate_tile(i, 0)
+            weigh(i, (0,))
+            quantise_weights(i + 1)
+            regroup(i + 2, W_SIDE)
+            leave(i - SUM_LAG)
+            gate_tile(i, 1)
+            weigh(i, (1,))
+            gate_tile(i, 2)
+            turn_c(t, (2, 3))
+            weigh(i, (2,))
+            combine(t - 1)
+            regroup(i + GATES, Z_SIDE, nc.scalar.copy)
+            gate_tile(i, 3)
+            weigh(i, (3,))
+            nc.scalar.activation(out=tanh_c[:, t - 1, :], in_=c_out[:, t - 1, :], func=ACT.Tanh)
+
+        def gg_unit(i):
+            gate_tile(i, 0)
+            leave(i - SUM_LAG)
+            fold_bones(i - 1)
+            quantise_weights(i + 1)
+            gate_tile(i, 1)
+            regroup(i + GATES, Z_SIDE)
+            regroup(i + 2, W_SIDE)
+            if i == GG_GATE:
+                regroup(i + 2, Z_SIDE)
+            if i + 2 < UNITS:
+                quantise_weights(i + 2)
+            gate_tile(i, 2)
+            gate_tile(i, 3)
+
+        def o_unit(i):
+            t = i // GATES
+            g_grouped = repeat_g(t + 1)
+            quantise_g(t + 1, g_grouped)
+            h_grouped = new_h_grouped()
+            turn_half(t + 1, 0, h_grouped)
+            gate_tile(i, 0)
+            fold_bones(i - 1)
+            gate_tile(i, 1)
+            turn_half(t + 1, 1, h_grouped)
+            for half in range(HALVES):
+                quantise_h(t + 1, h_grouped, half)
+            gate_tile(i, 2)
+            leave(i - SUM_LAG)
+            gate_tile(i, 3)
+            regroup(i + 2, W_SIDE)
+            regroup(i + GATES, Z_SIDE, nc.scalar.copy)
 
         for i in range(UNITS - 1):
             t, g = divmod(i, GATES)
@@ -337,63 +441,31 @@ def tile_st_hmr_pc_t_kernel(tc, h_new, c_new, g_s, c_g_s, Wg_s, Zg_s, bg_s, out_
                 for half in range(HALVES):
                     load_h(t + 1, half)
                 load_c(t + 1)
-            if i + AHEAD + 1 < UNITS:
-                load_weights(i + AHEAD + 1, range(2))
-
-            quantise_weights(i + 1)
-            if g == O_GATE:
-                h_grouped = new_h_grouped()
-                for half in range(HALVES):
-                    turn_half(t + 1, half, h_grouped)
-                g_grouped = repeat_g(t + 1)
-            if i >= SUM_LAG:
-                sum_bones(i - SUM_LAG, range(BANK_BONES), True, True)
-                finish(i - SUM_LAG)
-            if i + AHEAD < UNITS:
-                regroup_weights(i + AHEAD, 0, nc.vector.tensor_copy)
-                if g in Z_ON_SCALAR and i > 0:
-                    regroup_weights(i + AHEAD, 1, nc.scalar.copy)
-                else:
-                    regroup_weights(i + AHEAD, 1, nc.vector.tensor_copy)
-            if i >= 1:
-                fold_bones(i - 1)
-            if g == F_GATE and t >= 1:
-                combine(t - 1)
-            if g == O_GATE:
-                for half in range(HALVES):
-                    quantise_h(t + 1, h_grouped, half)
-                quantise_g(t + 1, g_grouped)
+            if i + GATES < UNITS:
+                load_weights(i + GATES, range(2))
             new_values(i)
-            first_tiles = 2 if i == 0 else 0
-            for x in range(first_tiles):
-                gate_tile(i, x)
-            if g == F_GATE:
-                turn_c(t)
-            for x in range(first_tiles, FEAT_TILES):
-                gate_tile(i, x)
-            if g == F_GATE:
-                for x in range(FEAT_TILES):
-                    weigh_by_c(i, x)
-                if t >= 1:
-                    nc.scalar.activation(out=tanh_c[:, t - 1, :], in_=c_out[:, t - 1, :], func=ACT.Tanh)
+            if i == 0:
+                first_unit()
+            else:
+                (f_unit, gg_unit, o_unit)[g](i)
 
         i = UNITS - 1
         t = FRAMES - 1
         fold_bones(i - 1)
-        sum_bones(i - SUM_LAG, range(BANK_BONES), True, True)
-        finish(i - SUM_LAG)
+        leave(i - SUM_LAG)
         store(out_0, g_out, 0, t)
         new_values(i)
         for half in range(HALVES):
-            pres = [multiply(i, x, half) for x in range(FEAT_TILES)]
+            pres = []
             pieces = LAST_SPLIT if half == HALVES - 1 else 1
             step = BANK_BONES // pieces
             for piece in range(pieces):
                 for x in range(FEAT_TILES):
+                    if piece == 0:
+                        pres.append(multiply(i, x, half, late=pieces > 1 and x >= 2))
                     squash(i, x, half, pres[x], slice(piece * step, (piece + 1) * step))
             if half == 0:
-                sum_bones(i - 1, range(BANK_BONES), True, True)
-                finish(i - 1)
+                leave(i - 1)
                 combine(t)
         nc.scalar.activation(out=tanh_c[:, t, :], in_=c_out[:, t, :], func=ACT.Tanh)
         store(out_1, c_out, 0, FRAMES)

@@ -105,7 +105,7 @@ def tile_st_hmr_pc_t_kernel(tc, h_new, c_new, g_s, c_g_s, Wg_s, Zg_s, bg_s, out_
 
         def regroup_weights(i, m, copy, cols=slice(0, FEAT)):
             if i not in wz_groupeds:
-                wz_grouped = stage.tile([P, 2, FEAT, PACK], BF16, align_bytes=64)
+                wz_grouped = stage.tile([P, 2, FEAT, PACK], BF16, align_bytes=64, bufs=3)
                 wz_groupeds[i] = wz_grouped
             copy(
                 out=wz_groupeds[i][:, m, cols].rearrange("q (c i) j -> q c j i", i=4),
@@ -262,6 +262,15 @@ def tile_st_hmr_pc_t_kernel(tc, h_new, c_new, g_s, c_g_s, Wg_s, Zg_s, bg_s, out_
                 op=ALU.mult,
             )
 
+        def fold_tile(i, x, engine):
+            values = gate_tiles[i]
+            engine.tensor_tensor(
+                out=values[:, 0:BANK_BONES, x, :],
+                in0=values[:, 0:BANK_BONES, x, :],
+                in1=values[:, BANK_BONES:BONES, x, :],
+                op=ALU.add,
+            )
+
         def fold_bones(i):
             values = gate_tiles[i]
             lower = values[:, 0:BANK_BONES].rearrange("p n x b -> p (n x b)")
@@ -362,6 +371,7 @@ def tile_st_hmr_pc_t_kernel(tc, h_new, c_new, g_s, c_g_s, Wg_s, Zg_s, bg_s, out_
         def weigh(i, tiles):
             for x in tiles:
                 weigh_by_c(i, x)
+                fold_tile(i, x, nc.gpsimd if x < 3 else nc.vector)
 
         def regroup(i, m, copy=nc.vector.tensor_copy):
             if i < UNITS:
@@ -385,14 +395,13 @@ def tile_st_hmr_pc_t_kernel(tc, h_new, c_new, g_s, c_g_s, Wg_s, Zg_s, bg_s, out_
         def f_unit(i):
             t = i // GATES
             turn_c(t, (0, 1))
+            quantise_weights(i + 1)
             fold_bones(i - 1)
             gate_tile(i, 0)
-            weigh(i, (0,))
-            quantise_weights(i + 1)
             regroup(i + 2, W_SIDE)
             leave(i - SUM_LAG)
             gate_tile(i, 1)
-            weigh(i, (1,))
+            weigh(i, (0, 1))
             gate_tile(i, 2)
             turn_c(t, (2, 3))
             weigh(i, (2,))
@@ -405,7 +414,6 @@ def tile_st_hmr_pc_t_kernel(tc, h_new, c_new, g_s, c_g_s, Wg_s, Zg_s, bg_s, out_
         def gg_unit(i):
             gate_tile(i, 0)
             leave(i - SUM_LAG)
-            fold_bones(i - 1)
             quantise_weights(i + 1)
             gate_tile(i, 1)
             regroup(i + GATES, Z_SIDE)
@@ -430,19 +438,20 @@ def tile_st_hmr_pc_t_kernel(tc, h_new, c_new, g_s, c_g_s, Wg_s, Zg_s, bg_s, out_
             for half in range(HALVES):
                 quantise_h(t + 1, h_grouped, half)
             gate_tile(i, 2)
-            leave(i - SUM_LAG)
             gate_tile(i, 3)
+            leave(i - SUM_LAG)
             regroup(i + 2, W_SIDE)
             regroup(i + GATES, Z_SIDE, nc.scalar.copy)
 
         for i in range(UNITS - 1):
             t, g = divmod(i, GATES)
+            if i + GATES < UNITS:
+                load_weights(i + GATES, range(2))
             if g == F_GATE and t + 1 < FRAMES:
                 for half in range(HALVES):
                     load_h(t + 1, half)
+            if g == GG_GATE and t + 1 < FRAMES:
                 load_c(t + 1)
-            if i + GATES < UNITS:
-                load_weights(i + GATES, range(2))
             new_values(i)
             if i == 0:
                 first_unit()

@@ -371,7 +371,8 @@ def tile_st_hmr_pc_t_kernel(tc, h_new, c_new, g_s, c_g_s, Wg_s, Zg_s, bg_s, out_
         def weigh(i, tiles):
             for x in tiles:
                 weigh_by_c(i, x)
-                fold_tile(i, x, nc.gpsimd if x < 3 else nc.vector)
+                if x < FEAT_TILES - 1:
+                    fold_tile(i, x, nc.gpsimd)
 
         def regroup(i, m, copy=nc.vector.tensor_copy):
             if i < UNITS:
@@ -379,13 +380,12 @@ def tile_st_hmr_pc_t_kernel(tc, h_new, c_new, g_s, c_g_s, Wg_s, Zg_s, bg_s, out_
 
         def first_unit():
             regroup(1, W_SIDE)
-            regroup(1, Z_SIDE)
             gate_tile(0, 0)
-            turn_c(0, (0, 1))
+            turn_c(0, range(FEAT_TILES))
+            regroup(1, Z_SIDE)
+            quantise_weights(1)
             gate_tile(0, 1)
             weigh(0, (0, 1))
-            turn_c(0, (2, 3))
-            quantise_weights(1)
             gate_tile(0, 2)
             regroup(2, W_SIDE)
             gate_tile(0, 3)
@@ -396,50 +396,50 @@ def tile_st_hmr_pc_t_kernel(tc, h_new, c_new, g_s, c_g_s, Wg_s, Zg_s, bg_s, out_
             t = i // GATES
             turn_c(t, (0, 1))
             quantise_weights(i + 1)
-            fold_bones(i - 1)
             gate_tile(i, 0)
-            regroup(i + 2, W_SIDE)
+            fold_bones(i - 1)
             leave(i - SUM_LAG)
             gate_tile(i, 1)
-            weigh(i, (0, 1))
+            weigh(i, (0,))
+            combine(t - 1)
             gate_tile(i, 2)
             turn_c(t, (2, 3))
-            weigh(i, (2,))
-            combine(t - 1)
             regroup(i + GATES, Z_SIDE, nc.scalar.copy)
             gate_tile(i, 3)
-            weigh(i, (3,))
+            weigh(i, (1, 2, 3))
             nc.scalar.activation(out=tanh_c[:, t - 1, :], in_=c_out[:, t - 1, :], func=ACT.Tanh)
 
         def gg_unit(i):
             gate_tile(i, 0)
             leave(i - SUM_LAG)
-            quantise_weights(i + 1)
             gate_tile(i, 1)
+            gate_tile(i, 2)
+            if i > GG_GATE:
+                regroup(i + 1, W_SIDE)
+            fold_tile(i - 1, FEAT_TILES - 1, nc.vector)
+            quantise_weights(i + 1)
+            gate_tile(i, 3)
             regroup(i + GATES, Z_SIDE)
             regroup(i + 2, W_SIDE)
             if i == GG_GATE:
                 regroup(i + 2, Z_SIDE)
-            if i + 2 < UNITS:
-                quantise_weights(i + 2)
-            gate_tile(i, 2)
-            gate_tile(i, 3)
 
         def o_unit(i):
             t = i // GATES
-            g_grouped = repeat_g(t + 1)
-            quantise_g(t + 1, g_grouped)
             h_grouped = new_h_grouped()
-            turn_half(t + 1, 0, h_grouped)
-            gate_tile(i, 0)
-            fold_bones(i - 1)
-            gate_tile(i, 1)
-            turn_half(t + 1, 1, h_grouped)
             for half in range(HALVES):
-                quantise_h(t + 1, h_grouped, half)
+                turn_half(t + 1, half, h_grouped)
+            quantise_h(t + 1, h_grouped, 0)
+            gate_tile(i, 0)
+            quantise_weights(i + 1)
+            g_grouped = repeat_g(t + 1)
+            gate_tile(i, 1)
+            quantise_g(t + 1, g_grouped)
+            fold_bones(i - 1)
             gate_tile(i, 2)
-            gate_tile(i, 3)
             leave(i - SUM_LAG)
+            gate_tile(i, 3)
+            quantise_h(t + 1, h_grouped, 1)
             regroup(i + 2, W_SIDE)
             regroup(i + GATES, Z_SIDE, nc.scalar.copy)
 

@@ -46,7 +46,7 @@ def tile_st_hmr_pc_t_kernel(tc, h_new, c_new, g_s, c_g_s, Wg_s, Zg_s, bg_s, out_
         raws = ctx.enter_context(tc.tile_pool(name="raws", bufs=GATES))
         stage = ctx.enter_context(tc.tile_pool(name="stage", bufs=2))
         frame_ops = ctx.enter_context(tc.tile_pool(name="frame_ops", bufs=2))
-        weight_ops = ctx.enter_context(tc.tile_pool(name="weight_ops", bufs=GATES + 1))
+        weight_ops = ctx.enter_context(tc.tile_pool(name="weight_ops", bufs=GATES))
         gate_pool = ctx.enter_context(tc.tile_pool(name="gate_pool", bufs=SUM_LAG + 2))
         mm = ctx.enter_context(tc.psum_pool(name="mm", bufs=MM_BANKS))
         flip = ctx.enter_context(tc.psum_pool(name="flip", bufs=8 - MM_BANKS))
@@ -105,7 +105,7 @@ def tile_st_hmr_pc_t_kernel(tc, h_new, c_new, g_s, c_g_s, Wg_s, Zg_s, bg_s, out_
 
         def regroup_weights(i, m, copy, cols=slice(0, FEAT)):
             if i not in wz_groupeds:
-                wz_grouped = stage.tile([P, 2, FEAT, PACK], BF16, align_bytes=64, bufs=3)
+                wz_grouped = stage.tile([P, 2, FEAT, PACK], BF16, align_bytes=64)
                 wz_groupeds[i] = wz_grouped
             copy(
                 out=wz_groupeds[i][:, m, cols].rearrange("q (c i) j -> q c j i", i=4),
@@ -374,74 +374,73 @@ def tile_st_hmr_pc_t_kernel(tc, h_new, c_new, g_s, c_g_s, Wg_s, Zg_s, bg_s, out_
                 if x < FEAT_TILES - 1:
                     fold_tile(i, x, nc.gpsimd)
 
-        def regroup(i, m, copy=nc.vector.tensor_copy):
+        regrouped = set()
+
+        def prepare(i):
             if i < UNITS:
-                regroup_weights(i, m, copy)
+                for m in range(2):
+                    if (i, m) not in regrouped:
+                        regroup_weights(i, m, nc.vector.tensor_copy)
+                quantise_weights(i)
+
+        def z_by_scalar(i):
+            regroup_weights(i, Z_SIDE, nc.scalar.copy)
+            regrouped.add((i, Z_SIDE))
 
         def first_unit():
-            regroup(1, W_SIDE)
             gate_tile(0, 0)
-            turn_c(0, range(FEAT_TILES))
-            regroup(1, Z_SIDE)
-            quantise_weights(1)
+            prepare(1)
+            turn_c(0, (0, 1))
             gate_tile(0, 1)
-            weigh(0, (0, 1))
+            weigh(0, (0,))
+            z_by_scalar(2)
+            turn_c(0, (2, 3))
             gate_tile(0, 2)
-            regroup(2, W_SIDE)
             gate_tile(0, 3)
-            weigh(0, (2, 3))
-            regroup(2, Z_SIDE, nc.scalar.copy)
+            weigh(0, (1, 2, 3))
 
         def f_unit(i):
             t = i // GATES
-            turn_c(t, (0, 1))
-            quantise_weights(i + 1)
-            gate_tile(i, 0)
-            fold_bones(i - 1)
+            prepare(i + 1)
             leave(i - SUM_LAG)
+            gate_tile(i, 0)
             gate_tile(i, 1)
-            weigh(i, (0,))
+            turn_c(t, (0, 1))
+            z_by_scalar(i + 2)
             combine(t - 1)
+            fold_bones(i - 1)
             gate_tile(i, 2)
-            turn_c(t, (2, 3))
-            regroup(i + GATES, Z_SIDE, nc.scalar.copy)
+            weigh(i, (0,))
             gate_tile(i, 3)
+            turn_c(t, (2, 3))
             weigh(i, (1, 2, 3))
             nc.scalar.activation(out=tanh_c[:, t - 1, :], in_=c_out[:, t - 1, :], func=ACT.Tanh)
 
         def gg_unit(i):
-            gate_tile(i, 0)
             leave(i - SUM_LAG)
+            gate_tile(i, 0)
             gate_tile(i, 1)
-            gate_tile(i, 2)
-            if i > GG_GATE:
-                regroup(i + 1, W_SIDE)
             fold_tile(i - 1, FEAT_TILES - 1, nc.vector)
-            quantise_weights(i + 1)
+            prepare(i + 1)
+            gate_tile(i, 2)
             gate_tile(i, 3)
-            regroup(i + GATES, Z_SIDE)
-            regroup(i + 2, W_SIDE)
-            if i == GG_GATE:
-                regroup(i + 2, Z_SIDE)
+            prepare(i + 2)
 
         def o_unit(i):
             t = i // GATES
             h_grouped = new_h_grouped()
             for half in range(HALVES):
                 turn_half(t + 1, half, h_grouped)
-            quantise_h(t + 1, h_grouped, 0)
             gate_tile(i, 0)
-            quantise_weights(i + 1)
+            fold_bones(i - 1)
             g_grouped = repeat_g(t + 1)
             gate_tile(i, 1)
             quantise_g(t + 1, g_grouped)
-            fold_bones(i - 1)
             gate_tile(i, 2)
             leave(i - SUM_LAG)
             gate_tile(i, 3)
-            quantise_h(t + 1, h_grouped, 1)
-            regroup(i + 2, W_SIDE)
-            regroup(i + GATES, Z_SIDE, nc.scalar.copy)
+            for half in range(HALVES):
+                quantise_h(t + 1, h_grouped, half)
 
         for i in range(UNITS - 1):
             t, g = divmod(i, GATES)

@@ -113,8 +113,8 @@ def tile_st_hmr_pc_t_kernel(tc, h_new, c_new, g_s, c_g_s, Wg_s, Zg_s, bg_s, out_
             )
 
         def quantise_weights(i):
-            wz_words = weight_ops.tile([P, 2 * FEAT], U32, align_bytes=64)
-            wz_scales = weight_ops.tile([P, 2 * FEAT], U8, align_bytes=64)
+            wz_words = weight_ops.tile([P, 2 * FEAT], U32, align_bytes=256)
+            wz_scales = weight_ops.tile([P, 2 * FEAT], U8, align_bytes=256)
             nc.vector.quantize_mx(
                 out=wz_words[:].bitcast(FP8X4),
                 scales=wz_scales[:],
@@ -124,8 +124,8 @@ def tile_st_hmr_pc_t_kernel(tc, h_new, c_new, g_s, c_g_s, Wg_s, Zg_s, bg_s, out_
 
         def quantise_part(i, m, cols):
             if i not in wz_ops:
-                wz_words = weight_ops.tile([P, 2 * FEAT], U32, align_bytes=64)
-                wz_scales = weight_ops.tile([P, 2 * FEAT], U8, align_bytes=64)
+                wz_words = weight_ops.tile([P, 2 * FEAT], U32, align_bytes=256)
+                wz_scales = weight_ops.tile([P, 2 * FEAT], U8, align_bytes=256)
                 wz_ops[i] = (wz_words, wz_scales)
             words, scales = wz_ops[i]
             op_cols = slice(m * FEAT + cols.start, m * FEAT + cols.stop)
@@ -171,8 +171,8 @@ def tile_st_hmr_pc_t_kernel(tc, h_new, c_new, g_s, c_g_s, Wg_s, Zg_s, bg_s, out_
 
         def quantise_h(t, h_grouped, half):
             if t not in h_ops:
-                h_words = frame_ops.tile([P, COLS], U32, align_bytes=64)
-                h_scales = frame_ops.tile([P, COLS], U8, align_bytes=64)
+                h_words = frame_ops.tile([P, COLS], U32, align_bytes=256)
+                h_scales = frame_ops.tile([P, COLS], U8, align_bytes=256)
                 h_ops[t] = (h_words, h_scales)
             words, scales = h_ops[t]
             cols = slice(half * BANK, (half + 1) * BANK)
@@ -183,8 +183,8 @@ def tile_st_hmr_pc_t_kernel(tc, h_new, c_new, g_s, c_g_s, Wg_s, Zg_s, bg_s, out_
             )
 
         def quantise_g(t, g_grouped):
-            g_words = frame_ops.tile([P, GROUP], U32, align_bytes=64)
-            g_scales = frame_ops.tile([P, GROUP], U8, align_bytes=64)
+            g_words = frame_ops.tile([P, GROUP], U32, align_bytes=256)
+            g_scales = frame_ops.tile([P, GROUP], U8, align_bytes=256)
             nc.vector.quantize_mx(out=g_words[:].bitcast(FP8X4), scales=g_scales[:], in_=g_grouped[:])
             g_ops[t] = (g_words, g_scales)
 
@@ -390,12 +390,12 @@ def tile_st_hmr_pc_t_kernel(tc, h_new, c_new, g_s, c_g_s, Wg_s, Zg_s, bg_s, out_
         def first_unit():
             gate_tile(0, 0)
             prepare(1)
-            turn_c(0, (0, 1))
             gate_tile(0, 1)
+            turn_c(0, (0, 1))
+            gate_tile(0, 2)
             weigh(0, (0,))
             z_by_scalar(2)
             turn_c(0, (2, 3))
-            gate_tile(0, 2)
             gate_tile(0, 3)
             weigh(0, (1, 2, 3))
 
@@ -429,12 +429,12 @@ def tile_st_hmr_pc_t_kernel(tc, h_new, c_new, g_s, c_g_s, Wg_s, Zg_s, bg_s, out_
         def o_unit(i):
             t = i // GATES
             h_grouped = new_h_grouped()
-            for half in range(HALVES):
-                turn_half(t + 1, half, h_grouped)
+            turn_half(t + 1, 0, h_grouped)
             gate_tile(i, 0)
             fold_bones(i - 1)
             g_grouped = repeat_g(t + 1)
             gate_tile(i, 1)
+            turn_half(t + 1, 1, h_grouped)
             quantise_g(t + 1, g_grouped)
             gate_tile(i, 2)
             leave(i - SUM_LAG)

from contextlib import ExitStack

import concourse.mybir as mybir
from concourse.masks import make_identity

F32 = mybir.dt.float32
BF16 = mybir.dt.bfloat16
U32 = mybir.dt.uint32
U8 = mybir.dt.uint8
FP8X4 = mybir.dt.float8_e4m3fn_x4
ACT = mybir.ActivationFunctionType
ALU = mybir.AluOpType

P = 128
PACK = 4
SEQS = 32
FRAMES = 4
BONES = 32
FEAT = 512
GATES = 3
F_GATE, GG_GATE, O_GATE = 0, 1, 2
W_SIDE, Z_SIDE = 0, 1
UNITS = FRAMES * GATES
FEAT_TILES = FEAT // P
BONE_ROWS = P // SEQS
BONE_STEPS = BONES // BONE_ROWS
WORDS = FEAT // 2
COLS = BONES * SEQS
BANK = 512
HALVES = COLS // BANK
BANK_BONES = BANK // SEQS
HALF_STEPS = BONE_STEPS // HALVES
SUM_LAG = 2
GROUP = 256
MM_BANKS = 4
LAST_SPLIT = 2

FLOPS = 2 * GATES * FRAMES * FEAT * FEAT * (COLS + SEQS)


def tile_st_hmr_pc_t_kernel(tc, h_new, c_new, g_s, c_g_s, Wg_s, Zg_s, bg_s, out_0, out_1):
    nc = tc.nc
    with ExitStack() as ctx:
        const = ctx.enter_context(tc.tile_pool(name="const", bufs=1))
        frames = ctx.enter_context(tc.tile_pool(name="frames", bufs=2))
        raws = ctx.enter_context(tc.tile_pool(name="raws", bufs=GATES))
        stage = ctx.enter_context(tc.tile_pool(name="stage", bufs=2))
        frame_ops = ctx.enter_context(tc.tile_pool(name="frame_ops", bufs=2))
        weight_ops = ctx.enter_context(tc.tile_pool(name="weight_ops", bufs=GATES))
        gate_pool = ctx.enter_context(tc.tile_pool(name="gate_pool", bufs=SUM_LAG + 2))
        mm = ctx.enter_context(tc.psum_pool(name="mm", bufs=MM_BANKS))
        flip = ctx.enter_context(tc.psum_pool(name="flip", bufs=8 - MM_BANKS))
        ctx.enter_context(tc.manual_schedule())

        warm = const.tile([P, 2], F32)
        nc.vector.memset(warm[:], 0.0)
        nc.scalar.activation(out=warm[:, 1:2], in_=warm[:, 0:1], func=ACT.Sigmoid)
        ident_f32 = const.tile([P, P], F32)
        make_identity(nc, ident_f32[:])
        ident_bf = const.tile([P, P], BF16)
        make_identity(nc, ident_bf[:])
        sort_f32 = const.tile([P, P], F32)
        nc.vector.tensor_copy(
            out=sort_f32[:].rearrange("i (r b) -> i r b", r=BONE_ROWS),
            in_=ident_f32[:].rearrange("i (b r) -> i r b", r=BONE_ROWS),
        )
        sort_bf = const.tile([P, P], BF16)
        nc.vector.tensor_copy(
            out=sort_bf[:].rearrange("i (r b) -> i r b", r=BONE_ROWS),
            in_=ident_bf[:].rearrange("i (b r) -> i r b", r=BONE_ROWS),
        )
        bias_rows = const.tile([P, P], BF16)
        nc.vector.memset(bias_rows[:], 0.0)

        h_raws, c_raws, wz_raws, wz_groupeds = {}, {}, {}, {}
        h_ops, g_ops, wz_ops, gate_tiles, c_turneds, totals = {}, {}, {}, {}, {}, {}

        def load_rows(raw, src, t, first_step, end_step):
            for r in range(BONE_ROWS):
                nc.sync.dma_start(
                    out=raw[r:P:BONE_ROWS, :],
                    in_=src[:, t, r * BONE_STEPS + first_step : r * BONE_STEPS + end_step, :].rearrange("b n k -> b (n k)"),
                )

        def load_h(t, half):
            h_raw = frames.tile([P, HALF_STEPS * FEAT], BF16, bufs=2 * HALVES)
            load_rows(h_raw, h_new, t, half * HALF_STEPS, (half + 1) * HALF_STEPS)
            h_raws[t, half] = h_raw

        def load_c(t):
            c_raw = frames.tile([P, BONE_STEPS * FEAT], BF16)
            load_rows(c_raw, c_new, t, 0, BONE_STEPS)
            c_raws[t] = c_raw

        def load_weights(i, matrices, cols=slice(0, FEAT)):
            t, g = divmod(i, GATES)
            if i not in wz_raws:
                wz_raw = raws.tile([P, 2, PACK, FEAT], BF16)
                wz_raws[i] = wz_raw
            for m in matrices:
                nc.sync.dma_start(
                    out=wz_raws[i][:, m, :, cols],
                    in_=(Wg_s, Zg_s)[m][g, t].rearrange("(q j) w -> q j w", j=PACK)[:, :, cols],
                )

        def regroup_weights(i, m, copy, cols=slice(0, FEAT)):
            if i not in wz_groupeds:
                wz_grouped = stage.tile([P, 2, FEAT, PACK], BF16, align_bytes=64)
                wz_groupeds[i] = wz_grouped
            copy(
                out=wz_groupeds[i][:, m, cols].rearrange("q (c i) j -> q c j i", i=4),
                in_=wz_raws[i][:, m, :, cols].rearrange("q j (c i) -> q c j i", i=4),
            )

        def quantise_weights(i):
            wz_words = weight_ops.tile([P, 2 * FEAT], U32, align_bytes=256)
            wz_scales = weight_ops.tile([P, 2 * FEAT], U8, align_bytes=256)
            nc.vector.quantize_mx(
                out=wz_words[:].bitcast(FP8X4),
                scales=wz_scales[:],
                in_=wz_groupeds[i][:].rearrange("q m w j -> q (m w j)"),
            )
            wz_ops[i] = (wz_words, wz_scales)

        def quantise_part(i, m, cols):
            if i not in wz_ops:
                wz_words = weight_ops.tile([P, 2 * FEAT], U32, align_bytes=256)
                wz_scales = weight_ops.tile([P, 2 * FEAT], U8, align_bytes=256)
                wz_ops[i] = (wz_words, wz_scales)
            words, scales = wz_ops[i]
            op_cols = slice(m * FEAT + cols.start, m * FEAT + cols.stop)
            nc.vector.quantize_mx(
                out=words[:, op_cols].bitcast(FP8X4),
                scales=scales[:, op_cols],
                in_=wz_groupeds[i][:, m, cols].rearrange("q w j -> q (w j)"),
            )

        def new_h_grouped():
            h_grouped = stage.tile([P, COLS * PACK], BF16, align_bytes=64)
            return h_grouped

        def turn_half(t, half, h_grouped):
            h_as_words = h_raws[t, half][:].bitcast(F32)
            h_grouped_words = h_grouped[:].bitcast(F32).rearrange("q (n c u) -> q n c u", c=P, u=2)
            for pair in range(HALF_STEPS // 2):
                turned = flip.tile([P, 2, 2, P], F32, tag="flip")
                for a in range(2):
                    first_word = (2 * pair + a) * WORDS
                    for u in range(2):
                        nc.tensor.transpose(
                            out=turned[:, a, u, :],
                            in_=h_as_words[:, first_word + u : first_word + WORDS : 2],
                            identity=sort_f32[:],
                        )
                step = half * HALF_STEPS + 2 * pair
                nc.scalar.copy(
                    out=h_grouped_words[:, step : step + 2],
                    in_=turned[:].rearrange("q a u c -> q a c u"),
                )

        def repeat_g(t):
            g_grouped = stage.tile([P, GROUP * PACK], BF16, align_bytes=64)
            nc.scalar.copy(
                out=g_grouped[:].bitcast(F32).rearrange("q (n b u) -> q n b u", b=SEQS, u=2),
                in_=g_sorted[:, :, t * SEQS : (t + 1) * SEQS]
                .rearrange("q u b -> q b u")
                .unsqueeze(1)
                .to_broadcast([P, GROUP // SEQS, SEQS, 2]),
            )
            return g_grouped

        def quantise_h(t, h_grouped, half):
            if t not in h_ops:
                h_words = frame_ops.tile([P, COLS], U32, align_bytes=256)
                h_scales = frame_ops.tile([P, COLS], U8, align_bytes=256)
                h_ops[t] = (h_words, h_scales)
            words, scales = h_ops[t]
            cols = slice(half * BANK, (half + 1) * BANK)
            nc.vector.quantize_mx(
                out=words[:, cols].bitcast(FP8X4),
                scales=scales[:, cols],
                in_=h_grouped[:, half * BANK * PACK : (half + 1) * BANK * PACK],
            )

        def quantise_g(t, g_grouped):
            g_words = frame_ops.tile([P, GROUP], U32, align_bytes=256)
            g_scales = frame_ops.tile([P, GROUP], U8, align_bytes=256)
            nc.vector.quantize_mx(out=g_words[:].bitcast(FP8X4), scales=g_scales[:], in_=g_grouped[:])
            g_ops[t] = (g_words, g_scales)

        def turn_c(t, tiles):
            for x in tiles:
                c_turned = flip.tile([P, COLS], BF16, tag="flip")
                for n in range(BONE_STEPS):
                    nc.tensor.matmul(
                        out=c_turned[:, n * P : (n + 1) * P],
                        lhsT=c_raws[t][:, n * FEAT + x * P : n * FEAT + (x + 1) * P],
                        rhs=sort_bf[:],
                        start=True,
                        stop=True,
                    )
                c_turneds[x] = c_turned

        def new_values(i):
            values = gate_pool.tile([P, BONES, FEAT_TILES, SEQS], F32)
            gate_tiles[i] = values

        def multiply(i, x, half, late=False):
            wz_words, wz_scales = wz_ops[i]
            h_words, h_scales = h_ops[i // GATES]
            g_words, g_scales = g_ops[i // GATES]
            w_cols = slice(x * P, (x + 1) * P)
            z_cols = slice(FEAT + x * P, FEAT + (x + 1) * P)
            if late:
                pre = flip.tile([P, BANK], F32, tag="flip")
            else:
                pre = mm.tile([P, BANK], F32)
            for first in range(0, BANK, GROUP):
                cols = slice(half * BANK + first, half * BANK + first + GROUP)
                nc.tensor.matmul_mx(
                    out=pre[:, first : first + GROUP],
                    lhsT=wz_words[:, w_cols].bitcast(FP8X4),
                    lhsT_scale=wz_scales[:, w_cols],
                    rhs=h_words[:, cols].bitcast(FP8X4),
                    rhs_scale=h_scales[:, cols],
                    start=True,
                    stop=False,
                )
                nc.tensor.matmul_mx(
                    out=pre[:, first : first + GROUP],
                    lhsT=wz_words[:, z_cols].bitcast(FP8X4),
                    lhsT_scale=wz_scales[:, z_cols],
                    rhs=g_words[:].bitcast(FP8X4),
                    rhs_scale=g_scales[:],
                    start=False,
                    stop=True,
                )
            return pre

        def squash(i, x, half, pre, bones):
            t, g = divmod(i, GATES)
            bias_col = (g * FRAMES + t) * FEAT_TILES + x
            nc.scalar.activation(
                out=gate_tiles[i][:, half * BANK_BONES + bones.start : half * BANK_BONES + bones.stop, x, :],
                in_=pre[:].rearrange("p (n b) -> p n b", b=SEQS)[:, bones],
                func=ACT.Sigmoid,
                bias=bias_cols[:, bias_col : bias_col + 1],
                scale=1.0,
            )

        def gate_tile(i, x):
            for half in range(HALVES):
                pre = multiply(i, x, half)
                squash(i, x, half, pre, slice(0, BANK_BONES))

        def weigh_by_c(i, x):
            values = gate_tiles[i]
            nc.vector.tensor_tensor(
                out=values[:, :, x, :],
                in0=values[:, :, x, :],
                in1=c_turneds.pop(x)[:].rearrange("p (n b) -> p n b", b=SEQS),
                op=ALU.mult,
            )

        def fold_tile(i, x, engine):
            values = gate_tiles[i]
            engine.tensor_tensor(
                out=values[:, 0:BANK_BONES, x, :],
                in0=values[:, 0:BANK_BONES, x, :],
                in1=values[:, BANK_BONES:BONES, x, :],
                op=ALU.add,
            )

        def fold_bones(i):
            values = gate_tiles[i]
            lower = values[:, 0:BANK_BONES].rearrange("p n x b -> p (n x b)")
            upper = values[:, BANK_BONES:BONES].rearrange("p n x b -> p (n x b)")
            nc.vector.tensor_tensor(out=lower, in0=lower, in1=upper, op=ALU.add)

        def sum_bones(i, bones, first, last):
            if first:
                total = flip.tile([P, P], F32, tag="flip")
                totals[i] = total
            for n in bones:
                nc.tensor.matmul(
                    out=totals[i][:],
                    lhsT=gate_tiles[i][:, n].rearrange("p x b -> p (x b)"),
                    rhs=ident_f32[:],
                    is_transpose=True,
                    start=(first and n == bones[0]),
                    stop=(last and n == bones[-1]),
                )

        def finish(i):
            t, g = divmod(i, GATES)
            if g == O_GATE:
                nc.vector.scalar_tensor_tensor(
                    out=g_out[:, t, :], in0=totals[i][:], scalar=1.0 / BONES, in1=tanh_c[:, t, :],
                    op0=ALU.mult, op1=ALU.mult,
                )
            else:
                nc.scalar.mul(out=means[:, g, t, :], in_=totals[i][:], mul=1.0 / BONES)

        def combine(t):
            nc.vector.tensor_tensor(out=c_out[:, t, :], in0=means[:, GG_GATE, t, :], in1=cg[:, t, :], op=ALU.mult)
            nc.vector.tensor_tensor(out=c_out[:, t, :], in0=c_out[:, t, :], in1=means[:, F_GATE, t, :], op=ALU.add)

        def store(dram, tile, first_t, end_t):
            for x in range(FEAT_TILES):
                nc.sync.dma_start(
                    out=dram[:, first_t:end_t, x * P : (x + 1) * P], in_=tile[x * SEQS : (x + 1) * SEQS, first_t:end_t]
                )

        g_raw = const.tile([P, FEAT], BF16)
        cg = const.tile([P, FRAMES, P], BF16)
        early, late = slice(0, FEAT // 2), slice(FEAT // 2, FEAT)
        load_h(0, 0)
        load_weights(0, range(2), early)
        nc.sync.dma_start(out=g_raw[:], in_=g_s.rearrange("b t k -> (b t) k"))
        nc.sync.dma_start(
            out=bias_rows[0 : UNITS * FEAT_TILES, :],
            in_=bg_s.rearrange("g t o (x p) -> (g t o x) p", p=P),
        )
        load_h(0, 1)
        load_weights(0, range(2), late)
        load_c(0)
        for i in range(1, GATES):
            load_weights(i, range(2))
        for x in range(FEAT_TILES):
            nc.sync.dma_start(out=cg[x * SEQS : (x + 1) * SEQS], in_=c_g_s[:, :, x * P : (x + 1) * P])

        means = const.tile([P, O_GATE, FRAMES, P], F32)
        c_out = const.tile([P, FRAMES, P], F32)
        tanh_c = const.tile([P, FRAMES, P], F32)
        g_out = const.tile([P, FRAMES, P], F32)

        h_grouped = new_h_grouped()
        turn_half(0, 0, h_grouped)
        g_turned = flip.tile([P, 2, P], F32, tag="flip")
        for u in range(2):
            nc.tensor.transpose(
                out=g_turned[:, u, :],
                in_=g_raw[:].bitcast(F32)[:, u:WORDS:2],
                identity=sort_f32[:],
            )
        g_sorted = const.tile([P, 2, P], F32)
        nc.scalar.copy(out=g_sorted[:], in_=g_turned[:])
        g_grouped = repeat_g(0)
        bias_turned = flip.tile([P, P], BF16, tag="flip")
        nc.tensor.transpose(out=bias_turned[:], in_=bias_rows[:], identity=ident_bf[:])
        bias_cols = const.tile([P, UNITS * FEAT_TILES], F32)
        turn_half(0, 1, h_grouped)

        for m in range(2):
            regroup_weights(0, m, nc.vector.tensor_copy, early)
        for m in range(2):
            quantise_part(0, m, early)
        quantise_h(0, h_grouped, 0)
        nc.vector.tensor_copy(out=bias_cols[:], in_=bias_turned[:, 0 : UNITS * FEAT_TILES])
        quantise_g(0, g_grouped)
        quantise_h(0, h_grouped, 1)
        for m in range(2):
            regroup_weights(0, m, nc.vector.tensor_copy, late)
        for m in range(2):
            quantise_part(0, m, late)
        def leave(i):
            if i >= 0:
                sum_bones(i, range(BANK_BONES), True, True)
                finish(i)

        def weigh(i, tiles):
            for x in tiles:
                weigh_by_c(i, x)
                if x < FEAT_TILES - 1:
                    fold_tile(i, x, nc.gpsimd)

        regrouped = set()

        def prepare(i):
            if i < UNITS:
                for m in range(2):
                    if (i, m) not in regrouped:
                        regroup_weights(i, m, nc.vector.tensor_copy)
                quantise_weights(i)

        def z_by_scalar(i):
            regroup_weights(i, Z_SIDE, nc.scalar.copy)
            regrouped.add((i, Z_SIDE))

        def first_unit():
            gate_tile(0, 0)
            prepare(1)
            gate_tile(0, 1)
            turn_c(0, (0, 1))
            gate_tile(0, 2)
            weigh(0, (0,))
            z_by_scalar(2)
            turn_c(0, (2, 3))
            gate_tile(0, 3)
            weigh(0, (1, 2, 3))

        def f_unit(i):
            t = i // GATES
            prepare(i + 1)
            leave(i - SUM_LAG)
            gate_tile(i, 0)
            gate_tile(i, 1)
            turn_c(t, (0, 1))
            z_by_scalar(i + 2)
            combine(t - 1)
            fold_bones(i - 1)
            gate_tile(i, 2)
            weigh(i, (0,))
            gate_tile(i, 3)
            turn_c(t, (2, 3))
            weigh(i, (1, 2, 3))
            nc.scalar.activation(out=tanh_c[:, t - 1, :], in_=c_out[:, t - 1, :], func=ACT.Tanh)

        def gg_unit(i):
            leave(i - SUM_LAG)
            gate_tile(i, 0)
            gate_tile(i, 1)
            fold_tile(i - 1, FEAT_TILES - 1, nc.vector)
            prepare(i + 1)
            gate_tile(i, 2)
            gate_tile(i, 3)
            prepare(i + 2)

        def o_unit(i):
            t = i // GATES
            h_grouped = new_h_grouped()
            turn_half(t + 1, 0, h_grouped)
            gate_tile(i, 0)
            fold_bones(i - 1)
            g_grouped = repeat_g(t + 1)
            gate_tile(i, 1)
            turn_half(t + 1, 1, h_grouped)
            quantise_g(t + 1, g_grouped)
            gate_tile(i, 2)
            leave(i - SUM_LAG)
            gate_tile(i, 3)
            for half in range(HALVES):
                quantise_h(t + 1, h_grouped, half)

        for i in range(UNITS - 1):
            t, g = divmod(i, GATES)
            if i + GATES < UNITS:
                load_weights(i + GATES, range(2))
            if g == F_GATE and t + 1 < FRAMES:
                for half in range(HALVES):
                    load_h(t + 1, half)
            if g == GG_GATE and t + 1 < FRAMES:
                load_c(t + 1)
            new_values(i)
            if i == 0:
                first_unit()
            else:
                (f_unit, gg_unit, o_unit)[g](i)

        i = UNITS - 1
        t = FRAMES - 1
        fold_bones(i - 1)
        leave(i - SUM_LAG)
        store(out_0, g_out, 0, t)
        new_values(i)
        for half in range(HALVES):
            pres = []
            pieces = LAST_SPLIT if half == HALVES - 1 else 1
            step = BANK_BONES // pieces
            for piece in range(pieces):
                for x in range(FEAT_TILES):
                    if piece == 0:
                        pres.append(multiply(i, x, half, late=pieces > 1 and x >= 2))
                    squash(i, x, half, pres[x], slice(piece * step, (piece + 1) * step))
            if half == 0:
                leave(i - 1)
                combine(t)
        nc.scalar.activation(out=tanh_c[:, t, :], in_=c_out[:, t, :], func=ACT.Tanh)
        store(out_1, c_out, 0, FRAMES)
        sum_bones(i, range(BONES), True, True)
        finish(i)
        store(out_0, g_out, t, FRAMES)
